import numpy as np
import ml_dtypes


def mxq(x, axis, fmt="e4m3"):
    dtype, down = {"e4m3": (ml_dtypes.float8_e4m3fn, 7), "e5m2": (ml_dtypes.float8_e5m2, 14)}[fmt]
    v = np.moveaxis(np.asarray(x, np.float32).astype(ml_dtypes.bfloat16).astype(np.float64), axis, -1)
    blocks = v.reshape(v.shape[:-1] + (-1, 32))
    amax = np.abs(blocks).max(-1, keepdims=True)
    byte = np.maximum(np.where(amax > 0, np.frexp(amax)[1] - 1 + 127, 0) - down, 1)
    scale = np.exp2(byte - 127.0)
    codes = (blocks / scale).astype(np.float32).astype(dtype).astype(np.float64)
    return np.moveaxis((codes * scale).reshape(v.shape), -1, axis)


WIDE = False


def mx_kscale(k):
    if not WIDE:
        return np.ones(k)
    levels = np.array([20, -20, 10, -10, 0])
    a = np.random.permutation(np.resize(levels, k // 512 * 4)).reshape(k // 512, 4)
    idx = np.arange(k)
    return np.exp2(a[idx // 512, idx % 128 // 32])


BF16 = ml_dtypes.bfloat16


def bf(x):
    return np.asarray(x, np.float32).astype(BF16)


def f64(x):
    return np.asarray(x).astype(np.float64)


B, IN, H = 2048, 512, 512


def sigmoid(v):
    return 1.0 / (1.0 + np.exp(-v))


def gru_parts(x, hidden, Wir_w, Wir_b, Whr_w, Whr_b, Wiz_w, Wiz_b, Whz_w, Whz_b, Win_w, Win_b, Whn_w, Whn_b):
    x, hidden = f64(x), f64(hidden)
    r = sigmoid(x @ f64(Wir_w).T + f64(Wir_b) + hidden @ f64(Whr_w).T + f64(Whr_b))
    z = sigmoid(x @ f64(Wiz_w).T + f64(Wiz_b) + hidden @ f64(Whz_w).T + f64(Whz_b))
    hn = hidden @ f64(Whn_w).T + f64(Whn_b)
    n = np.tanh(x @ f64(Win_w).T + f64(Win_b) + r * hn)
    return r, z, n, hn


def setup_inputs():
    u = mx_kscale(H)
    x = bf(np.random.standard_normal((B, IN)))
    hidden = bf(np.random.standard_normal((B, H)))
    p = {}
    for name, fan_in in (("Wir", IN), ("Whr", H), ("Wiz", IN), ("Whz", H), ("Win", IN), ("Whn", H)):
        p[name + "_w"] = bf(np.random.standard_normal((H, fan_in)) / np.sqrt(fan_in))
        p[name + "_b"] = bf(np.random.standard_normal(H) * 0.2)
    g = bf(np.random.standard_normal((B, H)) * np.exp2(np.random.randint(-12, 1, (B, 1))) * 16.0 * u[None, :])
    r, z, n, hn = gru_parts(x, hidden, **p)
    gates = np.concatenate([r, z, n], axis=1)
    for name in ("Wir", "Wiz", "Win"):
        p[name + "_w"] = bf(f64(p[name + "_w"]) / u[:, None])
    inp = {"x": x, "hidden": hidden}
    inp.update(p)
    inp["gates"] = np.asarray(gates, np.float32)
    inp["hn"] = np.asarray(hn, np.float32)
    inp["grad_out"] = g
    return inp


def reference(x, hidden, Wir_w, Wir_b, Whr_w, Whr_b, Wiz_w, Wiz_b, Whz_w, Whz_b, Win_w, Win_b, Whn_w, Whn_b, gates, hn, grad_out):
    g, h = f64(grad_out), f64(hidden)
    r, z, n = np.split(f64(gates), 3, axis=1)
    dn = g * (1.0 - z) * (1.0 - n * n)
    dz = g * (h - n) * z * (1.0 - z)
    dr = dn * f64(hn) * r * (1.0 - r)
    dgi = np.concatenate([dr, dz, dn], axis=1)
    Wi = np.concatenate([f64(Wir_w), f64(Wiz_w), f64(Win_w)], axis=0)
    return mxq(dgi, 1, "e5m2") @ mxq(Wi, 0, "e4m3")

@@ -1,0 +1,237 @@
+from contextlib import ExitStack
+
+import concourse.mybir as mybir
+from concourse.masks import make_identity
+
+F32 = mybir.dt.float32
+BF16 = mybir.dt.bfloat16
+U32 = mybir.dt.uint32
+U8 = mybir.dt.uint8
+E4M3X4 = mybir.dt.float8_e4m3fn_x4
+E5M2X4 = mybir.dt.float8_e5m2_x4
+ALU = mybir.AluOpType
+ACT = mybir.ActivationFunctionType
+
+P = 128
+PACK = 4
+B, H, IN = 2048, 512, 512
+TILES = 2
+CHUNKS = B // (P * TILES)
+WIDE = TILES * H
+WORDS = H // 2
+GATES = ("z", "n", "r")
+SAVED_COLUMN = {"r": 0, "z": 1, "n": 2}
+
+FLOPS = 2 * B * 3 * H * IN
+BYTES = 2 * (2 * B * H) + 3 * (2 * H * IN) + 4 * (3 * B * H) + 4 * (B * H) + 4 * (B * IN)
+
+
+def tile_gru_t_v_kernel(
+    tc,
+    x,
+    hidden,
+    Wir_w,
+    Wir_b,
+    Whr_w,
+    Whr_b,
+    Wiz_w,
+    Wiz_b,
+    Whz_w,
+    Whz_b,
+    Win_w,
+    Win_b,
+    Whn_w,
+    Whn_b,
+    gates,
+    hn,
+    grad_out,
+    out,
+):
+    nc = tc.nc
+    weight_of = {"r": Wir_w, "z": Wiz_w, "n": Win_w}
+
+    grad_view = grad_out.rearrange("(c p j) f -> c p j f", p=P, j=TILES)
+    hidden_view = hidden.rearrange("(c p j) f -> c p j f", p=P, j=TILES)
+    hn_view = hn.rearrange("(c p j) f -> c p j f", p=P, j=TILES)
+    gates_view = gates.rearrange("(c p j) (s f) -> c s p j f", p=P, j=TILES, s=3)
+    out_view = out.rearrange("(c p j) i -> c p j i", p=P, j=TILES)
+
+    with ExitStack() as ctx:
+        const = ctx.enter_context(tc.tile_pool(name="const", bufs=1))
+        stream = ctx.enter_context(tc.tile_pool(name="stream", bufs=3))
+        work = ctx.enter_context(tc.tile_pool(name="work", bufs=2))
+        psum_turn = ctx.enter_context(tc.psum_pool(name="psum_turn", bufs=4))
+        psum_sum = ctx.enter_context(tc.psum_pool(name="psum_sum", bufs=4))
+        ctx.enter_context(tc.manual_schedule())
+
+        ident = const.tile([P, P], F32)
+        make_identity(nc, ident[:])
+
+        w_raw = {}
+        w_grouped = {}
+        w_codes = {}
+        w_scales = {}
+
+        def load_weight(gate):
+            w_raw[gate] = const.tile([P, PACK, IN], BF16, name="w_raw_%s" % gate)
+            nc.sync.dma_start(
+                out=w_raw[gate][:].rearrange("p (u e) i -> p u (e i)", u=2),
+                in_=weight_of[gate].rearrange("(u p e) i -> p u (e i)", u=2, e=2),
+            )
+
+        def regroup_weight(gate):
+            w_grouped[gate] = const.tile(
+                [P, IN, PACK], BF16, name="w_grouped_%s" % gate, align_bytes=64
+            )
+            nc.scalar.copy(
+                out=w_grouped[gate][:], in_=w_raw[gate][:].rearrange("p t i -> p i t")
+            )
+
+        def quantise_weight(gate):
+            w_codes[gate] = const.tile([P, IN], U32, name="w_codes_%s" % gate, align_bytes=64)
+            w_scales[gate] = const.tile([P, IN], U8, name="w_scales_%s" % gate, align_bytes=64)
+            nc.vector.quantize_mx(
+                out=w_codes[gate][:].bitcast(E4M3X4),
+                scales=w_scales[gate][:],
+                in_=w_grouped[gate][:].rearrange("p i t -> p (i t)"),
+            )
+
+        def load(pool_tile, view):
+            nc.sync.dma_start(out=pool_tile[:].rearrange("p (j f) -> p j f", j=TILES), in_=view)
+
+        def load_chunk(c):
+            grad_in = stream.tile([P, WIDE], BF16)
+            load(grad_in, grad_view[c])
+            z_in = stream.tile([P, WIDE], F32)
+            load(z_in, gates_view[c, SAVED_COLUMN["z"]])
+            n_in = stream.tile([P, WIDE], F32)
+            load(n_in, gates_view[c, SAVED_COLUMN["n"]])
+            hidden_in = stream.tile([P, WIDE], BF16)
+            load(hidden_in, hidden_view[c])
+            hn_in = stream.tile([P, WIDE], F32)
+            load(hn_in, hn_view[c])
+            r_in = stream.tile([P, WIDE], F32)
+            load(r_in, gates_view[c, SAVED_COLUMN["r"]])
+            return {"grad": grad_in, "z": z_in, "n": n_in, "hidden": hidden_in, "hn": hn_in, "r": r_in}
+
+        def square_gates(chunk):
+            n_sq = work.tile([P, WIDE], F32)
+            nc.scalar.activation(out=n_sq[:], in_=chunk["n"][:], func=ACT.Square)
+            r_sq = work.tile([P, WIDE], F32)
+            nc.scalar.activation(out=r_sq[:], in_=chunk["r"][:], func=ACT.Square, bias=-0.5)
+            chunk["n_sq"] = n_sq
+            chunk["r_sq"] = r_sq
+
+        def turn_pairs(rounded, slot, grouped):
+            words = rounded[:].bitcast(F32)
+            turned = psum_turn.tile([P, TILES, 2, P], F32, tag="turned")
+            for j in range(TILES):
+                for u in range(2):
+                    first = (2 * j + u) * P
+                    nc.tensor.transpose(turned[:, j, u, :], words[:, first : first + P], ident[:])
+            nc.scalar.copy(
+                out=grouped[:]
+                .bitcast(F32)[:, slot * TILES * WORDS : (slot + 1) * TILES * WORDS]
+                .rearrange("p (j r u) -> p j r u", j=TILES, u=2),
+                in_=turned[:].rearrange("p j u r -> p j r u"),
+            )
+
+        def turn_float32(values, slot, grouped):
+            for j in range(TILES):
+                turned = psum_turn.tile([P, PACK, P], F32, tag="turned")
+                for u in range(2):
+                    for e in range(2):
+                        half = j * H + u * WORDS
+                        nc.tensor.transpose(
+                            turned[:, 2 * u + e, :], values[:, half + e : half + WORDS : 2], ident[:]
+                        )
+                first = (slot * TILES + j) * H
+                nc.scalar.copy(
+                    out=grouped[:, first : first + H].rearrange("p (r t) -> p r t", t=PACK),
+                    in_=turned[:].rearrange("p t r -> p r t"),
+                )
+
+        def multiply(c, grouped):
+            codes = work.tile([P, 3 * TILES * P], U32, align_bytes=64)
+            scales = work.tile([P, 3 * TILES * P], U8, align_bytes=64)
+            sums = [
+                psum_sum.tile([P, IN], F32, name="sums_%d" % j, tag="sums") for j in range(TILES)
+            ]
+            for slot, gate in enumerate(GATES):
+                cols = slice(slot * TILES * P, (slot + 1) * TILES * P)
+                nc.vector.quantize_mx(
+                    out=codes[:, cols].bitcast(E5M2X4),
+                    scales=scales[:, cols],
+                    in_=grouped[:, slot * WIDE : (slot + 1) * WIDE],
+                )
+                for j in range(TILES):
+                    tokens = slice((slot * TILES + j) * P, (slot * TILES + j + 1) * P)
+                    nc.tensor.matmul_mx(
+                        out=sums[j][:],
+                        lhsT=codes[:, tokens].bitcast(E5M2X4),
+                        lhsT_scale=scales[:, tokens],
+                        rhs=w_codes[gate][:].bitcast(E4M3X4),
+                        rhs_scale=w_scales[gate][:],
+                        start=(slot == 0),
+                        stop=(slot == len(GATES) - 1),
+                    )
+            result = work.tile([P, TILES * IN], F32)
+            for j in range(TILES):
+                nc.scalar.copy(out=result[:, j * IN : (j + 1) * IN], in_=sums[j][:])
+            nc.scalar.dma_start(
+                out=out_view[c], in_=result[:].rearrange("p (j i) -> p j i", j=TILES)
+            )
+
+        for gate in GATES:
+            load_weight(gate)
+        chunks = {0: load_chunk(0), 1: load_chunk(1)}
+        for gate in GATES:
+            regroup_weight(gate)
+        square_gates(chunks[0])
+
+        grouped_of = {}
+        for c in range(CHUNKS):
+            if c + 2 < CHUNKS:
+                chunks[c + 2] = load_chunk(c + 2)
+            t = chunks[c]
+            grouped = work.tile([P, 3 * WIDE], BF16, align_bytes=64)
+            grouped_of[c] = grouped
+
+            neg_a = work.tile([P, WIDE], F32)
+            nc.vector.scalar_tensor_tensor(
+                out=neg_a[:], in0=t["z"][:], scalar=1.0, in1=t["grad"][:], op0=ALU.subtract, op1=ALU.mult
+            )
+            neg_az = work.tile([P, WIDE], F32)
+            nc.vector.tensor_tensor(out=neg_az[:], in0=neg_a[:], in1=t["z"][:], op=ALU.mult)
+
+            if c + 1 < CHUNKS:
+                square_gates(chunks[c + 1])
+            if c > 0:
+                multiply(c - 1, grouped_of[c - 1])
+
+            n_less_h = work.tile([P, WIDE], F32)
+            nc.vector.tensor_tensor(out=n_less_h[:], in0=t["n"][:], in1=t["hidden"][:], op=ALU.subtract)
+            dz = work.tile([P, WIDE], BF16)
+            nc.vector.tensor_tensor(out=dz[:], in0=n_less_h[:], in1=neg_az[:], op=ALU.mult)
+            turn_pairs(dz, 0, grouped)
+
+            dn = work.tile([P, WIDE], F32)
+            nc.vector.scalar_tensor_tensor(
+                out=dn[:], in0=t["n_sq"][:], scalar=1.0, in1=neg_a[:], op0=ALU.subtract, op1=ALU.mult
+            )
+            turn_float32(dn, 1, grouped)
+
+            neg_dn_hn = work.tile([P, WIDE], F32)
+            nc.vector.scalar_tensor_tensor(
+                out=neg_dn_hn[:], in0=dn[:], scalar=-1.0, in1=t["hn"][:], op0=ALU.mult, op1=ALU.mult
+            )
+            dr = work.tile([P, WIDE], BF16)
+            nc.vector.scalar_tensor_tensor(
+                out=dr[:], in0=t["r_sq"][:], scalar=0.25, in1=neg_dn_hn[:], op0=ALU.subtract, op1=ALU.mult
+            )
+            turn_pairs(dr, 2, grouped)
+
+            if c == 0:
+                for gate in GATES:
+                    quantise_weight(gate)
+        multiply(CHUNKS - 1, grouped_of[CHUNKS - 1])

@@ -19,7 +19,7 @@ TILES = 2
 CHUNKS = B // (P * TILES)
 WIDE = TILES * H
 WORDS = H // 2
-GATES = ("z", "n", "r")
+GATES = ("n", "z", "r")
 SAVED_COLUMN = {"r": 0, "z": 1, "n": 2}
 
 FLOPS = 2 * B * 3 * H * IN
@@ -182,12 +182,13 @@ def tile_gru_t_v_kernel(
                 out=out_view[c], in_=result[:].rearrange("p (j i) -> p j i", j=TILES)
             )
 
+        chunks = {0: load_chunk(0)}
         for gate in GATES:
             load_weight(gate)
-        chunks = {0: load_chunk(0), 1: load_chunk(1)}
+        chunks[1] = load_chunk(1)
+        square_gates(chunks[0])
         for gate in GATES:
             regroup_weight(gate)
-        square_gates(chunks[0])
 
         grouped_of = {}
         for c in range(CHUNKS):
@@ -201,37 +202,36 @@ def tile_gru_t_v_kernel(
             nc.vector.scalar_tensor_tensor(
                 out=neg_a[:], in0=t["z"][:], scalar=1.0, in1=t["grad"][:], op0=ALU.subtract, op1=ALU.mult
             )
-            neg_az = work.tile([P, WIDE], F32)
-            nc.vector.tensor_tensor(out=neg_az[:], in0=neg_a[:], in1=t["z"][:], op=ALU.mult)
-
-            if c + 1 < CHUNKS:
-                square_gates(chunks[c + 1])
-            if c > 0:
-                multiply(c - 1, grouped_of[c - 1])
-
             n_less_h = work.tile([P, WIDE], F32)
             nc.vector.tensor_tensor(out=n_less_h[:], in0=t["n"][:], in1=t["hidden"][:], op=ALU.subtract)
-            dz = work.tile([P, WIDE], BF16)
-            nc.vector.tensor_tensor(out=dz[:], in0=n_less_h[:], in1=neg_az[:], op=ALU.mult)
-            turn_pairs(dz, 0, grouped)
-
+            neg_az = work.tile([P, WIDE], F32)
+            nc.vector.tensor_tensor(out=neg_az[:], in0=neg_a[:], in1=t["z"][:], op=ALU.mult)
             dn = work.tile([P, WIDE], F32)
             nc.vector.scalar_tensor_tensor(
                 out=dn[:], in0=t["n_sq"][:], scalar=1.0, in1=neg_a[:], op0=ALU.subtract, op1=ALU.mult
             )
-            turn_float32(dn, 1, grouped)
+            if c + 1 < CHUNKS:
+                square_gates(chunks[c + 1])
+            turn_float32(dn, 0, grouped)
+
+            dz = work.tile([P, WIDE], BF16)
+            nc.vector.tensor_tensor(out=dz[:], in0=n_less_h[:], in1=neg_az[:], op=ALU.mult)
+            turn_pairs(dz, 1, grouped)
 
             neg_dn_hn = work.tile([P, WIDE], F32)
             nc.vector.scalar_tensor_tensor(
                 out=neg_dn_hn[:], in0=dn[:], scalar=-1.0, in1=t["hn"][:], op0=ALU.mult, op1=ALU.mult
             )
+
+            if c == 1:
+                for gate in GATES:
+                    quantise_weight(gate)
+            if c > 0:
+                multiply(c - 1, grouped_of[c - 1])
+
             dr = work.tile([P, WIDE], BF16)
             nc.vector.scalar_tensor_tensor(
                 out=dr[:], in0=t["r_sq"][:], scalar=0.25, in1=neg_dn_hn[:], op0=ALU.subtract, op1=ALU.mult
             )
             turn_pairs(dr, 2, grouped)
-
-            if c == 0:
-                for gate in GATES:
-                    quantise_weight(gate)
         multiply(CHUNKS - 1, grouped_of[CHUNKS - 1])

@@ -15,15 +15,22 @@ ACT = mybir.ActivationFunctionType
 P = 128
 PACK = 4
 B, H, IN = 2048, 512, 512
-TILES = 2
-CHUNKS = B // (P * TILES)
-WIDE = TILES * H
 WORDS = H // 2
 GATES = ("n", "z", "r")
 SAVED_COLUMN = {"r": 0, "z": 1, "n": 2}
 
+TILES = 2
+CHUNK_TILES = [TILES] * (B // (P * TILES) - 1) + [1] * TILES
+CHUNKS = len(CHUNK_TILES)
+FIRST_TOKEN = [P * sum(CHUNK_TILES[:c]) for c in range(CHUNKS)]
+
 FLOPS = 2 * B * 3 * H * IN
 BYTES = 2 * (2 * B * H) + 3 * (2 * H * IN) + 4 * (3 * B * H) + 4 * (B * H) + 4 * (B * IN)
+
+
+def tokens_of(tensor, c):
+    rows = tensor[FIRST_TOKEN[c] : FIRST_TOKEN[c] + P * CHUNK_TILES[c], :]
+    return rows.rearrange("(p j) f -> p j f", j=CHUNK_TILES[c])
 
 
 def tile_gru_t_v_kernel(
@@ -50,19 +57,12 @@ def tile_gru_t_v_kernel(
     nc = tc.nc
     weight_of = {"r": Wir_w, "z": Wiz_w, "n": Win_w}
 
-    grad_view = grad_out.rearrange("(c p j) f -> c p j f", p=P, j=TILES)
-    hidden_view = hidden.rearrange("(c p j) f -> c p j f", p=P, j=TILES)
-    hn_view = hn.rearrange("(c p j) f -> c p j f", p=P, j=TILES)
-    gates_view = gates.rearrange("(c p j) (s f) -> c s p j f", p=P, j=TILES, s=3)
-    out_view = out.rearrange("(c p j) i -> c p j i", p=P, j=TILES)
-
     with ExitStack() as ctx:
         const = ctx.enter_context(tc.tile_pool(name="const", bufs=1))
         stream = ctx.enter_context(tc.tile_pool(name="stream", bufs=3))
         work = ctx.enter_context(tc.tile_pool(name="work", bufs=2))
         psum_turn = ctx.enter_context(tc.psum_pool(name="psum_turn", bufs=4))
         psum_sum = ctx.enter_context(tc.psum_pool(name="psum_sum", bufs=4))
-        ctx.enter_context(tc.manual_schedule())
 
         ident = const.tile([P, P], F32)
         make_identity(nc, ident[:])
@@ -96,48 +96,58 @@ def tile_gru_t_v_kernel(
                 in_=w_grouped[gate][:].rearrange("p i t -> p (i t)"),
             )
 
-        def load(pool_tile, view):
-            nc.sync.dma_start(out=pool_tile[:].rearrange("p (j f) -> p j f", j=TILES), in_=view)
-
         def load_chunk(c):
-            grad_in = stream.tile([P, WIDE], BF16)
-            load(grad_in, grad_view[c])
-            z_in = stream.tile([P, WIDE], F32)
-            load(z_in, gates_view[c, SAVED_COLUMN["z"]])
-            n_in = stream.tile([P, WIDE], F32)
-            load(n_in, gates_view[c, SAVED_COLUMN["n"]])
-            hidden_in = stream.tile([P, WIDE], BF16)
-            load(hidden_in, hidden_view[c])
-            hn_in = stream.tile([P, WIDE], F32)
-            load(hn_in, hn_view[c])
-            r_in = stream.tile([P, WIDE], F32)
-            load(r_in, gates_view[c, SAVED_COLUMN["r"]])
+            tiles = CHUNK_TILES[c]
+            wide = tiles * H
+
+            def load(sbuf_tile, view):
+                nc.sync.dma_start(
+                    out=sbuf_tile[:].rearrange("p (j f) -> p j f", j=tiles), in_=view
+                )
+
+            def saved(gate):
+                first = SAVED_COLUMN[gate] * H
+                return tokens_of(gates, c)[:, :, first : first + H]
+
+            grad_in = stream.tile([P, wide], BF16)
+            load(grad_in, tokens_of(grad_out, c))
+            z_in = stream.tile([P, wide], F32)
+            load(z_in, saved("z"))
+            n_in = stream.tile([P, wide], F32)
+            load(n_in, saved("n"))
+            hidden_in = stream.tile([P, wide], BF16)
+            load(hidden_in, tokens_of(hidden, c))
+            hn_in = stream.tile([P, wide], F32)
+            load(hn_in, tokens_of(hn, c))
+            r_in = stream.tile([P, wide], F32)
+            load(r_in, saved("r"))
             return {"grad": grad_in, "z": z_in, "n": n_in, "hidden": hidden_in, "hn": hn_in, "r": r_in}
 
-        def square_gates(chunk):
-            n_sq = work.tile([P, WIDE], F32)
-            nc.scalar.activation(out=n_sq[:], in_=chunk["n"][:], func=ACT.Square)
-            r_sq = work.tile([P, WIDE], F32)
-            nc.scalar.activation(out=r_sq[:], in_=chunk["r"][:], func=ACT.Square, bias=-0.5)
-            chunk["n_sq"] = n_sq
-            chunk["r_sq"] = r_sq
+        def square_gates(c):
+            wide = CHUNK_TILES[c] * H
+            n_sq = work.tile([P, wide], F32)
+            nc.scalar.activation(out=n_sq[:], in_=chunks[c]["n"][:], func=ACT.Square)
+            r_sq = work.tile([P, wide], F32)
+            nc.scalar.activation(out=r_sq[:], in_=chunks[c]["r"][:], func=ACT.Square, bias=-0.5)
+            chunks[c]["n_sq"] = n_sq
+            chunks[c]["r_sq"] = r_sq
 
-        def turn_pairs(rounded, slot, grouped):
+        def turn_pairs(rounded, slot, grouped, tiles):
             words = rounded[:].bitcast(F32)
-            turned = psum_turn.tile([P, TILES, 2, P], F32, tag="turned")
-            for j in range(TILES):
+            turned = psum_turn.tile([P, tiles, 2, P], F32, tag="turned")
+            for j in range(tiles):
                 for u in range(2):
                     first = (2 * j + u) * P
                     nc.tensor.transpose(turned[:, j, u, :], words[:, first : first + P], ident[:])
             nc.scalar.copy(
                 out=grouped[:]
-                .bitcast(F32)[:, slot * TILES * WORDS : (slot + 1) * TILES * WORDS]
-                .rearrange("p (j r u) -> p j r u", j=TILES, u=2),
+                .bitcast(F32)[:, slot * tiles * WORDS : (slot + 1) * tiles * WORDS]
+                .rearrange("p (j r u) -> p j r u", j=tiles, u=2),
                 in_=turned[:].rearrange("p j u r -> p j r u"),
             )
 
-        def turn_float32(values, slot, grouped):
-            for j in range(TILES):
+        def turn_float32(values, slot, grouped, tiles):
+            for j in range(tiles):
                 turned = psum_turn.tile([P, PACK, P], F32, tag="turned")
                 for u in range(2):
                     for e in range(2):
@@ -145,27 +155,29 @@ def tile_gru_t_v_kernel(
                         nc.tensor.transpose(
                             turned[:, 2 * u + e, :], values[:, half + e : half + WORDS : 2], ident[:]
                         )
-                first = (slot * TILES + j) * H
+                first = (slot * tiles + j) * H
                 nc.scalar.copy(
                     out=grouped[:, first : first + H].rearrange("p (r t) -> p r t", t=PACK),
                     in_=turned[:].rearrange("p t r -> p r t"),
                 )
 
-        def multiply(c, grouped):
-            codes = work.tile([P, 3 * TILES * P], U32, align_bytes=64)
-            scales = work.tile([P, 3 * TILES * P], U8, align_bytes=64)
+        def multiply(c):
+            tiles = CHUNK_TILES[c]
+            grouped = chunks[c]["grouped"]
+            codes = work.tile([P, 3 * tiles * P], U32, align_bytes=64)
+            scales = work.tile([P, 3 * tiles * P], U8, align_bytes=64)
             sums = [
-                psum_sum.tile([P, IN], F32, name="sums_%d" % j, tag="sums") for j in range(TILES)
+                psum_sum.tile([P, IN], F32, name="sums_%d" % j, tag="sums") for j in range(tiles)
             ]
             for slot, gate in enumerate(GATES):
-                cols = slice(slot * TILES * P, (slot + 1) * TILES * P)
+                cols = slice(slot * tiles * P, (slot + 1) * tiles * P)
                 nc.vector.quantize_mx(
                     out=codes[:, cols].bitcast(E5M2X4),
                     scales=scales[:, cols],
-                    in_=grouped[:, slot * WIDE : (slot + 1) * WIDE],
+                    in_=grouped[:, slot * tiles * H : (slot + 1) * tiles * H],
                 )
-                for j in range(TILES):
-                    tokens = slice((slot * TILES + j) * P, (slot * TILES + j + 1) * P)
+                for j in range(tiles):
+                    tokens = slice((slot * tiles + j) * P, (slot * tiles + j + 1) * P)
                     nc.tensor.matmul_mx(
                         out=sums[j][:],
                         lhsT=codes[:, tokens].bitcast(E5M2X4),
@@ -175,50 +187,51 @@ def tile_gru_t_v_kernel(
                         start=(slot == 0),
                         stop=(slot == len(GATES) - 1),
                     )
-            result = work.tile([P, TILES * IN], F32)
-            for j in range(TILES):
+            result = work.tile([P, tiles * IN], F32)
+            for j in range(tiles):
                 nc.scalar.copy(out=result[:, j * IN : (j + 1) * IN], in_=sums[j][:])
             nc.scalar.dma_start(
-                out=out_view[c], in_=result[:].rearrange("p (j i) -> p j i", j=TILES)
+                out=tokens_of(out, c), in_=result[:].rearrange("p (j i) -> p j i", j=tiles)
             )
 
         chunks = {0: load_chunk(0)}
         for gate in GATES:
             load_weight(gate)
         chunks[1] = load_chunk(1)
-        square_gates(chunks[0])
+        square_gates(0)
         for gate in GATES:
             regroup_weight(gate)
 
-        grouped_of = {}
         for c in range(CHUNKS):
             if c + 2 < CHUNKS:
                 chunks[c + 2] = load_chunk(c + 2)
             t = chunks[c]
-            grouped = work.tile([P, 3 * WIDE], BF16, align_bytes=64)
-            grouped_of[c] = grouped
+            tiles = CHUNK_TILES[c]
+            wide = tiles * H
+            grouped = work.tile([P, 3 * wide], BF16, align_bytes=64)
+            t["grouped"] = grouped
 
-            neg_a = work.tile([P, WIDE], F32)
+            neg_a = work.tile([P, wide], F32)
             nc.vector.scalar_tensor_tensor(
                 out=neg_a[:], in0=t["z"][:], scalar=1.0, in1=t["grad"][:], op0=ALU.subtract, op1=ALU.mult
             )
-            n_less_h = work.tile([P, WIDE], F32)
+            n_less_h = work.tile([P, wide], F32)
             nc.vector.tensor_tensor(out=n_less_h[:], in0=t["n"][:], in1=t["hidden"][:], op=ALU.subtract)
-            neg_az = work.tile([P, WIDE], F32)
+            neg_az = work.tile([P, wide], F32)
             nc.vector.tensor_tensor(out=neg_az[:], in0=neg_a[:], in1=t["z"][:], op=ALU.mult)
-            dn = work.tile([P, WIDE], F32)
+            dn = work.tile([P, wide], F32)
             nc.vector.scalar_tensor_tensor(
                 out=dn[:], in0=t["n_sq"][:], scalar=1.0, in1=neg_a[:], op0=ALU.subtract, op1=ALU.mult
             )
             if c + 1 < CHUNKS:
-                square_gates(chunks[c + 1])
-            turn_float32(dn, 0, grouped)
+                square_gates(c + 1)
+            turn_float32(dn, 0, grouped, tiles)
 
-            dz = work.tile([P, WIDE], BF16)
+            dz = work.tile([P, wide], BF16)
             nc.vector.tensor_tensor(out=dz[:], in0=n_less_h[:], in1=neg_az[:], op=ALU.mult)
-            turn_pairs(dz, 1, grouped)
+            turn_pairs(dz, 1, grouped, tiles)
 
-            neg_dn_hn = work.tile([P, WIDE], F32)
+            neg_dn_hn = work.tile([P, wide], F32)
             nc.vector.scalar_tensor_tensor(
                 out=neg_dn_hn[:], in0=dn[:], scalar=-1.0, in1=t["hn"][:], op0=ALU.mult, op1=ALU.mult
             )
@@ -227,11 +240,11 @@ def tile_gru_t_v_kernel(
                 for gate in GATES:
                     quantise_weight(gate)
             if c > 0:
-                multiply(c - 1, grouped_of[c - 1])
+                multiply(c - 1)
 
-            dr = work.tile([P, WIDE], BF16)
+            dr = work.tile([P, wide], BF16)
             nc.vector.scalar_tensor_tensor(
                 out=dr[:], in0=t["r_sq"][:], scalar=0.25, in1=neg_dn_hn[:], op0=ALU.subtract, op1=ALU.mult
             )
-            turn_pairs(dr, 2, grouped)
-        multiply(CHUNKS - 1, grouped_of[CHUNKS - 1])
+            turn_pairs(dr, 2, grouped, tiles)
+        multiply(CHUNKS - 1)

@@ -63,6 +63,7 @@ def tile_gru_t_v_kernel(
         work = ctx.enter_context(tc.tile_pool(name="work", bufs=2))
         psum_turn = ctx.enter_context(tc.psum_pool(name="psum_turn", bufs=4))
         psum_sum = ctx.enter_context(tc.psum_pool(name="psum_sum", bufs=4))
+        ctx.enter_context(tc.manual_schedule())
 
         ident = const.tile([P, P], F32)
         make_identity(nc, ident[:])

@@ -62,11 +62,13 @@ def tile_gru_t_v_kernel(
         stream = ctx.enter_context(tc.tile_pool(name="stream", bufs=3))
         work = ctx.enter_context(tc.tile_pool(name="work", bufs=2))
         psum_turn = ctx.enter_context(tc.psum_pool(name="psum_turn", bufs=4))
-        psum_sum = ctx.enter_context(tc.psum_pool(name="psum_sum", bufs=4))
-        ctx.enter_context(tc.manual_schedule())
+        psum_sum = ctx.enter_context(tc.psum_pool(name="psum_sum", bufs=2))
+        psum_grad = ctx.enter_context(tc.psum_pool(name="psum_grad", bufs=2))
 
         ident = const.tile([P, P], F32)
         make_identity(nc, ident[:])
+        ident_bf16 = const.tile([P, P], BF16)
+        make_identity(nc, ident_bf16[:])
 
         w_raw = {}
         w_grouped = {}
@@ -213,11 +215,24 @@ def tile_gru_t_v_kernel(
             t["grouped"] = grouped
 
             neg_a = work.tile([P, wide], F32)
-            nc.vector.scalar_tensor_tensor(
-                out=neg_a[:], in0=t["z"][:], scalar=1.0, in1=t["grad"][:], op0=ALU.subtract, op1=ALU.mult
-            )
+            for j in range(tiles):
+                cols = slice(j * H, (j + 1) * H)
+                grad_psum = psum_grad.tile([P, H], F32)
+                nc.tensor.matmul(
+                    out=grad_psum[:], lhsT=ident_bf16[:], rhs=t["grad"][:, cols], start=True, stop=True
+                )
+                nc.vector.scalar_tensor_tensor(
+                    out=neg_a[:, cols], in0=t["z"][:, cols], scalar=1.0, in1=grad_psum[:],
+                    op0=ALU.subtract, op1=ALU.mult,
+                )
             n_less_h = work.tile([P, wide], F32)
-            nc.vector.tensor_tensor(out=n_less_h[:], in0=t["n"][:], in1=t["hidden"][:], op=ALU.subtract)
+            nc.vector.tensor_tensor(
+                out=n_less_h[:, :H], in0=t["n"][:, :H], in1=t["hidden"][:, :H], op=ALU.subtract
+            )
+            if tiles > 1:
+                nc.gpsimd.tensor_tensor(
+                    out=n_less_h[:, H:], in0=t["n"][:, H:], in1=t["hidden"][:, H:], op=ALU.subtract
+                )
             neg_az = work.tile([P, wide], F32)
             nc.vector.tensor_tensor(out=neg_az[:], in0=neg_a[:], in1=t["z"][:], op=ALU.mult)
             dn = work.tile([P, wide], F32)

@@ -15,22 +15,30 @@ ACT = mybir.ActivationFunctionType
 P = 128
 PACK = 4
 B, H, IN = 2048, 512, 512
-WORDS = H // 2
-GATES = ("n", "z", "r")
-SAVED_COLUMN = {"r": 0, "z": 1, "n": 2}
+TILES = B // P
+GATES = ("n", "r", "z")
 
-TILES = 2
-CHUNK_TILES = [TILES] * (B // (P * TILES) - 1) + [1] * TILES
-CHUNKS = len(CHUNK_TILES)
-FIRST_TOKEN = [P * sum(CHUNK_TILES[:c]) for c in range(CHUNKS)]
+CHUNKS = [1, 1] + [2] * 7
+GROUPS = [2] * 7 + [1, 1]
+AHEAD = 2
+LOADS_AHEAD = 3
+
+FIRST_TILE = [sum(CHUNKS[:c]) for c in range(len(CHUNKS))]
+CHUNK_OF = [c for c in range(len(CHUNKS)) for j in range(CHUNKS[c])]
+FIRST_OF = [sum(GROUPS[:g]) for g in range(len(GROUPS))]
+GROUP_OF = [g for g in range(len(GROUPS)) for m in range(GROUPS[g])]
 
 FLOPS = 2 * B * 3 * H * IN
 BYTES = 2 * (2 * B * H) + 3 * (2 * H * IN) + 4 * (3 * B * H) + 4 * (B * H) + 4 * (B * IN)
 
 
 def tokens_of(tensor, c):
-    rows = tensor[FIRST_TOKEN[c] : FIRST_TOKEN[c] + P * CHUNK_TILES[c], :]
-    return rows.rearrange("(p j) f -> p j f", j=CHUNK_TILES[c])
+    rows = tensor[FIRST_TILE[c] * P : (FIRST_TILE[c] + CHUNKS[c]) * P, :]
+    return rows.rearrange("(p j) f -> p j f", j=CHUNKS[c])
+
+
+def place(i):
+    return CHUNK_OF[i], i - FIRST_TILE[CHUNK_OF[i]]
 
 
 def tile_gru_t_v_kernel(
@@ -59,11 +67,13 @@ def tile_gru_t_v_kernel(
 
     with ExitStack() as ctx:
         const = ctx.enter_context(tc.tile_pool(name="const", bufs=1))
-        stream = ctx.enter_context(tc.tile_pool(name="stream", bufs=3))
-        work = ctx.enter_context(tc.tile_pool(name="work", bufs=2))
-        psum_turn = ctx.enter_context(tc.psum_pool(name="psum_turn", bufs=4))
+        stream = ctx.enter_context(tc.tile_pool(name="stream", bufs=4))
+        natural = ctx.enter_context(tc.tile_pool(name="natural", bufs=4))
+        turned = ctx.enter_context(tc.tile_pool(name="turned", bufs=3))
+        packed = ctx.enter_context(tc.tile_pool(name="packed", bufs=2))
+        psum_turn = ctx.enter_context(tc.psum_pool(name="psum_turn", bufs=5))
+        psum_grad = ctx.enter_context(tc.psum_pool(name="psum_grad", bufs=1))
         psum_sum = ctx.enter_context(tc.psum_pool(name="psum_sum", bufs=2))
-        psum_grad = ctx.enter_context(tc.psum_pool(name="psum_grad", bufs=2))
 
         ident = const.tile([P, P], F32)
         make_identity(nc, ident[:])
@@ -74,20 +84,13 @@ def tile_gru_t_v_kernel(
         w_grouped = {}
         w_codes = {}
         w_scales = {}
-
-        def load_weight(gate):
+        for gate in GATES:
             w_raw[gate] = const.tile([P, PACK, IN], BF16, name="w_raw_%s" % gate)
             nc.sync.dma_start(
-                out=w_raw[gate][:].rearrange("p (u e) i -> p u (e i)", u=2),
-                in_=weight_of[gate].rearrange("(u p e) i -> p u (e i)", u=2, e=2),
+                out=w_raw[gate][:], in_=weight_of[gate].rearrange("(t p) i -> p t i", t=PACK)
             )
-
-        def regroup_weight(gate):
             w_grouped[gate] = const.tile(
                 [P, IN, PACK], BF16, name="w_grouped_%s" % gate, align_bytes=64
-            )
-            nc.scalar.copy(
-                out=w_grouped[gate][:], in_=w_raw[gate][:].rearrange("p t i -> p i t")
             )
 
         def quantise_weight(gate):
@@ -99,168 +102,190 @@ def tile_gru_t_v_kernel(
                 in_=w_grouped[gate][:].rearrange("p i t -> p (i t)"),
             )
 
+        loaded = {}
+
         def load_chunk(c):
-            tiles = CHUNK_TILES[c]
-            wide = tiles * H
+            size = CHUNKS[c]
+            grad_in = stream.tile([P, size, H], BF16)
+            gates_in = stream.tile([P, size, 3 * H], F32)
+            hidden_in = stream.tile([P, size, H], BF16)
+            hn_in = stream.tile([P, size, H], F32)
+            if c == 0:
+                nc.sync.dma_start(out=gates_in[:, :, 0:H], in_=tokens_of(gates, c)[:, :, 0:H])
+                nc.sync.dma_start(out=hn_in[:], in_=tokens_of(hn, c))
+                nc.sync.dma_start(out=grad_in[:], in_=tokens_of(grad_out, c))
+                nc.sync.dma_start(out=gates_in[:, :, H : 3 * H], in_=tokens_of(gates, c)[:, :, H : 3 * H])
+                nc.sync.dma_start(out=hidden_in[:], in_=tokens_of(hidden, c))
+            else:
+                nc.sync.dma_start(out=grad_in[:], in_=tokens_of(grad_out, c))
+                nc.sync.dma_start(out=gates_in[:], in_=tokens_of(gates, c))
+                nc.sync.dma_start(out=hidden_in[:], in_=tokens_of(hidden, c))
+                nc.sync.dma_start(out=hn_in[:], in_=tokens_of(hn, c))
+            loaded[c] = {"grad": grad_in, "gates": gates_in, "hidden": hidden_in, "hn": hn_in}
 
-            def load(sbuf_tile, view):
-                nc.sync.dma_start(
-                    out=sbuf_tile[:].rearrange("p (j f) -> p j f", j=tiles), in_=view
-                )
+        for c in range(LOADS_AHEAD):
+            load_chunk(c)
 
-            def saved(gate):
-                first = SAVED_COLUMN[gate] * H
-                return tokens_of(gates, c)[:, :, first : first + H]
+        nc.vector.tensor_copy(out=w_grouped["n"][:], in_=w_raw["n"][:].rearrange("p t i -> p i t"))
+        nc.vector.tensor_copy(out=w_grouped["r"][:], in_=w_raw["r"][:].rearrange("p t i -> p i t"))
+        half = IN // 2
+        nc.scalar.copy(
+            out=w_grouped["z"][:, :half, :], in_=w_raw["z"][:, :, :half].rearrange("p t i -> p i t")
+        )
+        nc.gpsimd.tensor_scalar(
+            out=w_grouped["z"][:, half:, :],
+            in0=w_raw["z"][:, :, half:].rearrange("p t i -> p i t"),
+            scalar1=1.0,
+            scalar2=0.0,
+            op0=ALU.mult,
+            op1=ALU.add,
+        )
+        for gate in GATES:
+            quantise_weight(gate)
 
-            grad_in = stream.tile([P, wide], BF16)
-            load(grad_in, tokens_of(grad_out, c))
-            z_in = stream.tile([P, wide], F32)
-            load(z_in, saved("z"))
-            n_in = stream.tile([P, wide], F32)
-            load(n_in, saved("n"))
-            hidden_in = stream.tile([P, wide], BF16)
-            load(hidden_in, tokens_of(hidden, c))
-            hn_in = stream.tile([P, wide], F32)
-            load(hn_in, tokens_of(hn, c))
-            r_in = stream.tile([P, wide], F32)
-            load(r_in, saved("r"))
-            return {"grad": grad_in, "z": z_in, "n": n_in, "hidden": hidden_in, "hn": hn_in, "r": r_in}
+        made = {}
+        grad_turned = {}
 
-        def square_gates(c):
-            wide = CHUNK_TILES[c] * H
-            n_sq = work.tile([P, wide], F32)
-            nc.scalar.activation(out=n_sq[:], in_=chunks[c]["n"][:], func=ACT.Square)
-            r_sq = work.tile([P, wide], F32)
-            nc.scalar.activation(out=r_sq[:], in_=chunks[c]["r"][:], func=ACT.Square, bias=-0.5)
-            chunks[c]["n_sq"] = n_sq
-            chunks[c]["r_sq"] = r_sq
+        def prepare(i):
+            c, j = place(i)
+            t = loaded[c]
+            r_in = t["gates"][:, j, 0:H]
+            n_in = t["gates"][:, j, 2 * H : 3 * H]
+            r_sq = natural.tile([P, H], F32)
+            nc.scalar.activation(out=r_sq[:], in_=r_in, func=ACT.Square, bias=-0.5)
+            r_slope = natural.tile([P, H], F32)
+            nc.scalar.activation(out=r_slope[:], in_=r_sq[:], func=ACT.Copy, bias=0.25, scale=-1.0)
+            hn_slope = natural.tile([P, H], F32)
+            nc.gpsimd.tensor_tensor(out=hn_slope[:], in0=t["hn"][:, j, :], in1=r_slope[:], op=ALU.mult)
+            n_sq = natural.tile([P, H], F32)
+            nc.scalar.activation(out=n_sq[:], in_=n_in, func=ACT.Square)
+            n_less_h = natural.tile([P, H], F32)
+            nc.gpsimd.tensor_tensor(out=n_less_h[:], in0=n_in, in1=t["hidden"][:, j, :], op=ALU.subtract)
+            made[i] = {"n_sq": n_sq, "n_less_h": n_less_h, "hn_slope": hn_slope}
 
-        def turn_pairs(rounded, slot, grouped, tiles):
-            words = rounded[:].bitcast(F32)
-            turned = psum_turn.tile([P, tiles, 2, P], F32, tag="turned")
-            for j in range(tiles):
-                for u in range(2):
-                    first = (2 * j + u) * P
-                    nc.tensor.transpose(turned[:, j, u, :], words[:, first : first + P], ident[:])
-            nc.scalar.copy(
-                out=grouped[:]
-                .bitcast(F32)[:, slot * tiles * WORDS : (slot + 1) * tiles * WORDS]
-                .rearrange("p (j r u) -> p j r u", j=tiles, u=2),
-                in_=turned[:].rearrange("p j u r -> p j r u"),
-            )
-
-        def turn_float32(values, slot, grouped, tiles):
-            for j in range(tiles):
-                turned = psum_turn.tile([P, PACK, P], F32, tag="turned")
-                for u in range(2):
-                    for e in range(2):
-                        half = j * H + u * WORDS
-                        nc.tensor.transpose(
-                            turned[:, 2 * u + e, :], values[:, half + e : half + WORDS : 2], ident[:]
-                        )
-                first = (slot * tiles + j) * H
-                nc.scalar.copy(
-                    out=grouped[:, first : first + H].rearrange("p (r t) -> p r t", t=PACK),
-                    in_=turned[:].rearrange("p t r -> p r t"),
-                )
-
-        def multiply(c):
-            tiles = CHUNK_TILES[c]
-            grouped = chunks[c]["grouped"]
-            codes = work.tile([P, 3 * tiles * P], U32, align_bytes=64)
-            scales = work.tile([P, 3 * tiles * P], U8, align_bytes=64)
-            sums = [
-                psum_sum.tile([P, IN], F32, name="sums_%d" % j, tag="sums") for j in range(tiles)
-            ]
-            for slot, gate in enumerate(GATES):
-                cols = slice(slot * tiles * P, (slot + 1) * tiles * P)
-                nc.vector.quantize_mx(
-                    out=codes[:, cols].bitcast(E5M2X4),
-                    scales=scales[:, cols],
-                    in_=grouped[:, slot * tiles * H : (slot + 1) * tiles * H],
-                )
-                for j in range(tiles):
-                    tokens = slice((slot * tiles + j) * P, (slot * tiles + j + 1) * P)
-                    nc.tensor.matmul_mx(
-                        out=sums[j][:],
-                        lhsT=codes[:, tokens].bitcast(E5M2X4),
-                        lhsT_scale=scales[:, tokens],
-                        rhs=w_codes[gate][:].bitcast(E4M3X4),
-                        rhs_scale=w_scales[gate][:],
-                        start=(slot == 0),
-                        stop=(slot == len(GATES) - 1),
+        def turn_grad(c):
+            bank = psum_grad.tile([P, CHUNKS[c], PACK, P], BF16)
+            for j in range(CHUNKS[c]):
+                for t in range(PACK):
+                    nc.tensor.transpose(
+                        bank[:, j, t, :], loaded[c]["grad"][:, j, t * P : (t + 1) * P], ident_bf16[:]
                     )
-            result = work.tile([P, tiles * IN], F32)
-            for j in range(tiles):
-                nc.scalar.copy(out=result[:, j * IN : (j + 1) * IN], in_=sums[j][:])
-            nc.scalar.dma_start(
-                out=tokens_of(out, c), in_=result[:].rearrange("p (j i) -> p j i", j=tiles)
-            )
+            grad_t = turned.tile([P, CHUNKS[c], P, PACK], BF16)
+            nc.scalar.copy(out=grad_t[:], in_=bank[:].rearrange("p j t c -> p j c t"))
+            grad_turned[c] = grad_t
 
-        chunks = {0: load_chunk(0)}
-        for gate in GATES:
-            load_weight(gate)
-        chunks[1] = load_chunk(1)
-        square_gates(0)
-        for gate in GATES:
-            regroup_weight(gate)
+        def turn(values):
+            bank = psum_turn.tile([P, PACK, P], F32, tag="bank")
+            for t in range(PACK):
+                nc.tensor.transpose(bank[:, t, :], values[:, t * P : (t + 1) * P], ident[:])
+            return bank[:].rearrange("p t c -> p c t")
 
-        for c in range(CHUNKS):
-            if c + 2 < CHUNKS:
-                chunks[c + 2] = load_chunk(c + 2)
-            t = chunks[c]
-            tiles = CHUNK_TILES[c]
-            wide = tiles * H
-            grouped = work.tile([P, 3 * wide], BF16, align_bytes=64)
-            t["grouped"] = grouped
+        def z_of(i):
+            c, j = place(i)
+            return loaded[c]["gates"][:, j, H : 2 * H]
 
-            neg_a = work.tile([P, wide], F32)
-            for j in range(tiles):
-                cols = slice(j * H, (j + 1) * H)
-                grad_psum = psum_grad.tile([P, H], F32)
-                nc.tensor.matmul(
-                    out=grad_psum[:], lhsT=ident_bf16[:], rhs=t["grad"][:, cols], start=True, stop=True
+        grouped = {}
+        codes = {}
+        scales = {}
+
+        def slot(i, gate):
+            g = GROUP_OF[i]
+            return GATES.index(gate) * GROUPS[g] + i - FIRST_OF[g]
+
+        def grouped_at(i, gate):
+            s = slot(i, gate)
+            return grouped[GROUP_OF[i]][:, s * H : (s + 1) * H].rearrange("p (c t) -> p c t", t=PACK)
+
+        def quantise(g):
+            n = GROUPS[g]
+            codes[g] = packed.tile([P, 3 * n * P], U32, name="codes", align_bytes=64)
+            scales[g] = packed.tile([P, 3 * n * P], U8, name="scales", align_bytes=64)
+            for a, b in ((0, 2 * n), (2 * n, 3 * n)):
+                nc.vector.quantize_mx(
+                    out=codes[g][:, a * P : b * P].bitcast(E5M2X4),
+                    scales=scales[g][:, a * P : b * P],
+                    in_=grouped[g][:, a * H : b * H],
                 )
-                nc.vector.scalar_tensor_tensor(
-                    out=neg_a[:, cols], in0=t["z"][:, cols], scalar=1.0, in1=grad_psum[:],
-                    op0=ALU.subtract, op1=ALU.mult,
+
+        def multiply(i):
+            g = GROUP_OF[i]
+            c, j = place(i)
+            sums = psum_sum.tile([P, IN], F32)
+            for gate in GATES:
+                s = slot(i, gate)
+                nc.tensor.matmul_mx(
+                    out=sums[:],
+                    lhsT=codes[g][:, s * P : (s + 1) * P].bitcast(E5M2X4),
+                    lhsT_scale=scales[g][:, s * P : (s + 1) * P],
+                    rhs=w_codes[gate][:].bitcast(E4M3X4),
+                    rhs_scale=w_scales[gate][:],
+                    start=(gate == GATES[0]),
+                    stop=(gate == GATES[-1]),
                 )
-            n_less_h = work.tile([P, wide], F32)
-            nc.vector.tensor_tensor(
-                out=n_less_h[:, :H], in0=t["n"][:, :H], in1=t["hidden"][:, :H], op=ALU.subtract
-            )
-            if tiles > 1:
-                nc.gpsimd.tensor_tensor(
-                    out=n_less_h[:, H:], in0=t["n"][:, H:], in1=t["hidden"][:, H:], op=ALU.subtract
-                )
-            neg_az = work.tile([P, wide], F32)
-            nc.vector.tensor_tensor(out=neg_az[:], in0=neg_a[:], in1=t["z"][:], op=ALU.mult)
-            dn = work.tile([P, wide], F32)
+            result = packed.tile([P, IN], F32, name="result")
+            nc.scalar.copy(out=result[:], in_=sums[:])
+            nc.scalar.dma_start(out=tokens_of(out, c)[:, j, :], in_=result[:])
+
+        def finish_z(i, bank, neg_az):
+            nc.vector.tensor_tensor(out=grouped_at(i, "z"), in0=bank, in1=neg_az[:], op=ALU.mult)
+
+        turn_grad(0)
+        prepare(0)
+        banks = {0: {"z": turn(z_of(0))}}
+        banks[0]["n_sq"] = turn(made[0]["n_sq"][:])
+        banks[0]["hn_slope"] = turn(made[0]["hn_slope"][:])
+        banks[0]["n_less_h"] = turn(made[0]["n_less_h"][:])
+        for i in range(1, AHEAD):
+            prepare(i)
+
+        multiplied = 0
+        quantised = 0
+        waiting = {}
+        for i in range(TILES):
+            c, j = place(i)
+            g = GROUP_OF[i]
+            more = i + 1 < TILES
+            if j == 0 and c + LOADS_AHEAD < len(CHUNKS):
+                load_chunk(c + LOADS_AHEAD)
+            if more and place(i + 1)[1] == 0:
+                turn_grad(c + 1)
+            if i + AHEAD < TILES:
+                prepare(i + AHEAD)
+            if i == FIRST_OF[g]:
+                grouped[g] = packed.tile([P, 3 * GROUPS[g] * H], BF16, name="grouped", align_bytes=64)
+            here = banks[i]
+
+            neg_a = turned.tile([P, P, PACK], F32)
             nc.vector.scalar_tensor_tensor(
-                out=dn[:], in0=t["n_sq"][:], scalar=1.0, in1=neg_a[:], op0=ALU.subtract, op1=ALU.mult
+                out=neg_a[:], in0=here["z"], scalar=1.0, in1=grad_turned[c][:, j, :, :],
+                op0=ALU.subtract, op1=ALU.mult,
             )
-            if c + 1 < CHUNKS:
-                square_gates(c + 1)
-            turn_float32(dn, 0, grouped, tiles)
-
-            dz = work.tile([P, wide], BF16)
-            nc.vector.tensor_tensor(out=dz[:], in0=n_less_h[:], in1=neg_az[:], op=ALU.mult)
-            turn_pairs(dz, 1, grouped, tiles)
-
-            neg_dn_hn = work.tile([P, wide], F32)
+            if i > 0:
+                finish_z(i - 1, banks[i - 1]["n_less_h"], waiting[i - 1])
+            if more:
+                banks[i + 1] = {"z": turn(z_of(i + 1))}
+            dn = turned.tile([P, P, PACK], F32)
             nc.vector.scalar_tensor_tensor(
-                out=neg_dn_hn[:], in0=dn[:], scalar=-1.0, in1=t["hn"][:], op0=ALU.mult, op1=ALU.mult
+                out=dn[:], in0=here["n_sq"], scalar=1.0, in1=neg_a[:], op0=ALU.subtract, op1=ALU.mult
             )
-
-            if c == 1:
-                for gate in GATES:
-                    quantise_weight(gate)
-            if c > 0:
-                multiply(c - 1)
-
-            dr = work.tile([P, wide], BF16)
-            nc.vector.scalar_tensor_tensor(
-                out=dr[:], in0=t["r_sq"][:], scalar=0.25, in1=neg_dn_hn[:], op0=ALU.subtract, op1=ALU.mult
-            )
-            turn_pairs(dr, 2, grouped, tiles)
-        multiply(CHUNKS - 1)
+            nc.scalar.copy(out=grouped_at(i, "n"), in_=dn[:])
+            if more:
+                banks[i + 1]["n_sq"] = turn(made[i + 1]["n_sq"][:])
+            if i == FIRST_OF[g] and g > 0:
+                quantise(g - 1)
+                quantised = i
+            for m in range(multiplied, quantised if not more else min(quantised, multiplied + 1)):
+                multiply(m)
+                multiplied = m + 1
+            neg_az = turned.tile([P, P, PACK], F32)
+            nc.vector.tensor_tensor(out=neg_az[:], in0=here["z"], in1=neg_a[:], op=ALU.mult)
+            waiting[i] = neg_az
+            if more:
+                banks[i + 1]["hn_slope"] = turn(made[i + 1]["hn_slope"][:])
+            nc.vector.tensor_tensor(out=grouped_at(i, "r"), in0=here["hn_slope"], in1=dn[:], op=ALU.mult)
+            if more:
+                banks[i + 1]["n_less_h"] = turn(made[i + 1]["n_less_h"][:])
+        finish_z(TILES - 1, banks[TILES - 1]["n_less_h"], waiting[TILES - 1])
+        quantise(len(GROUPS) - 1)
+        for m in range(multiplied, TILES):
+            multiply(m)

@@ -79,6 +79,10 @@ def tile_gru_t_v_kernel(
         make_identity(nc, ident[:])
         ident_bf16 = const.tile([P, P], BF16)
         make_identity(nc, ident_bf16[:])
+        neg_ident_bf16 = const.tile([P, P], BF16)
+        nc.vector.tensor_scalar(
+            out=neg_ident_bf16[:], in0=ident_bf16[:], scalar1=-1.0, scalar2=0.0, op0=ALU.mult, op1=ALU.add
+        )
 
         w_raw = {}
         w_grouped = {}
@@ -154,14 +158,14 @@ def tile_gru_t_v_kernel(
             r_sq = natural.tile([P, H], F32)
             nc.scalar.activation(out=r_sq[:], in_=r_in, func=ACT.Square, bias=-0.5)
             r_slope = natural.tile([P, H], F32)
-            nc.scalar.activation(out=r_slope[:], in_=r_sq[:], func=ACT.Copy, bias=0.25, scale=-1.0)
+            nc.gpsimd.tensor_scalar(
+                out=r_slope[:], in0=r_sq[:], scalar1=-1.0, scalar2=0.25, op0=ALU.mult, op1=ALU.add
+            )
             hn_slope = natural.tile([P, H], F32)
             nc.gpsimd.tensor_tensor(out=hn_slope[:], in0=t["hn"][:, j, :], in1=r_slope[:], op=ALU.mult)
             n_sq = natural.tile([P, H], F32)
             nc.scalar.activation(out=n_sq[:], in_=n_in, func=ACT.Square)
-            n_less_h = natural.tile([P, H], F32)
-            nc.gpsimd.tensor_tensor(out=n_less_h[:], in0=n_in, in1=t["hidden"][:, j, :], op=ALU.subtract)
-            made[i] = {"n_sq": n_sq, "n_less_h": n_less_h, "hn_slope": hn_slope}
+            made[i] = {"n_sq": n_sq, "hn_slope": hn_slope}
 
         def turn_grad(c):
             bank = psum_grad.tile([P, CHUNKS[c], PACK, P], BF16)
@@ -178,6 +182,21 @@ def tile_gru_t_v_kernel(
             bank = psum_turn.tile([P, PACK, P], F32, tag="bank")
             for t in range(PACK):
                 nc.tensor.transpose(bank[:, t, :], values[:, t * P : (t + 1) * P], ident[:])
+            return bank[:].rearrange("p t c -> p c t")
+
+        def turn_n_less_h(i):
+            c, j = place(i)
+            bank = psum_turn.tile([P, PACK, P], F32, tag="bank")
+            for t in range(PACK):
+                cols = slice(t * P, (t + 1) * P)
+                nc.tensor.matmul(
+                    out=bank[:, t, :], lhsT=loaded[c]["gates"][:, j, 2 * H + t * P : 2 * H + (t + 1) * P],
+                    rhs=ident[:], is_transpose=True, start=True, stop=False,
+                )
+                nc.tensor.matmul(
+                    out=bank[:, t, :], lhsT=loaded[c]["hidden"][:, j, cols], rhs=neg_ident_bf16[:],
+                    start=False, stop=True,
+                )
             return bank[:].rearrange("p t c -> p c t")
 
         def z_of(i):
@@ -234,7 +253,7 @@ def tile_gru_t_v_kernel(
         banks = {0: {"z": turn(z_of(0))}}
         banks[0]["n_sq"] = turn(made[0]["n_sq"][:])
         banks[0]["hn_slope"] = turn(made[0]["hn_slope"][:])
-        banks[0]["n_less_h"] = turn(made[0]["n_less_h"][:])
+        banks[0]["n_less_h"] = turn_n_less_h(0)
         for i in range(1, AHEAD):
             prepare(i)
 
@@ -284,7 +303,7 @@ def tile_gru_t_v_kernel(
                 banks[i + 1]["hn_slope"] = turn(made[i + 1]["hn_slope"][:])
             nc.vector.tensor_tensor(out=grouped_at(i, "r"), in0=here["hn_slope"], in1=dn[:], op=ALU.mult)
             if more:
-                banks[i + 1]["n_less_h"] = turn(made[i + 1]["n_less_h"][:])
+                banks[i + 1]["n_less_h"] = turn_n_less_h(i + 1)
         finish_z(TILES - 1, banks[TILES - 1]["n_less_h"], waiting[TILES - 1])
         quantise(len(GROUPS) - 1)
         for m in range(multiplied, TILES):

@@ -18,15 +18,14 @@ B, H, IN = 2048, 512, 512
 TILES = B // P
 GATES = ("n", "r", "z")
 
-CHUNKS = [1, 1] + [2] * 7
-GROUPS = [2] * 7 + [1, 1]
-AHEAD = 2
-LOADS_AHEAD = 3
+CHUNKS = [1, 1, 1, 1] + [2] * 6
+BLOCKS = [2, 2] + [4] * 10 + [2, 1, 1]
+STREAM_BUFS = 5
 
 FIRST_TILE = [sum(CHUNKS[:c]) for c in range(len(CHUNKS))]
 CHUNK_OF = [c for c in range(len(CHUNKS)) for j in range(CHUNKS[c])]
-FIRST_OF = [sum(GROUPS[:g]) for g in range(len(GROUPS))]
-GROUP_OF = [g for g in range(len(GROUPS)) for m in range(GROUPS[g])]
+FIRST_UNIT = [sum(BLOCKS[:b]) for b in range(len(BLOCKS))]
+BLOCK_OF = [b for b in range(len(BLOCKS)) for u in range(BLOCKS[b])]
 
 FLOPS = 2 * B * 3 * H * IN
 BYTES = 2 * (2 * B * H) + 3 * (2 * H * IN) + 4 * (3 * B * H) + 4 * (B * H) + 4 * (B * IN)
@@ -66,13 +65,16 @@ def tile_gru_t_v_kernel(
     weight_of = {"r": Wir_w, "z": Wiz_w, "n": Win_w}
 
     with ExitStack() as ctx:
+        ctx.enter_context(tc.manual_schedule())
         const = ctx.enter_context(tc.tile_pool(name="const", bufs=1))
-        stream = ctx.enter_context(tc.tile_pool(name="stream", bufs=4))
-        natural = ctx.enter_context(tc.tile_pool(name="natural", bufs=4))
+        stream = ctx.enter_context(tc.tile_pool(name="stream", bufs=STREAM_BUFS))
+        natural = ctx.enter_context(tc.tile_pool(name="natural", bufs=2))
+        single = ctx.enter_context(tc.tile_pool(name="single", bufs=1))
         turned = ctx.enter_context(tc.tile_pool(name="turned", bufs=3))
-        packed = ctx.enter_context(tc.tile_pool(name="packed", bufs=2))
-        psum_turn = ctx.enter_context(tc.psum_pool(name="psum_turn", bufs=5))
-        psum_grad = ctx.enter_context(tc.psum_pool(name="psum_grad", bufs=1))
+        packed = ctx.enter_context(tc.tile_pool(name="packed", bufs=3))
+        results = ctx.enter_context(tc.tile_pool(name="results", bufs=4))
+        psum_z = ctx.enter_context(tc.psum_pool(name="psum_z", bufs=2))
+        psum_one = ctx.enter_context(tc.psum_pool(name="psum_one", bufs=1))
         psum_sum = ctx.enter_context(tc.psum_pool(name="psum_sum", bufs=2))
 
         ident = const.tile([P, P], F32)
@@ -121,190 +123,256 @@ def tile_gru_t_v_kernel(
                 nc.sync.dma_start(out=gates_in[:, :, H : 3 * H], in_=tokens_of(gates, c)[:, :, H : 3 * H])
                 nc.sync.dma_start(out=hidden_in[:], in_=tokens_of(hidden, c))
             else:
-                nc.sync.dma_start(out=grad_in[:], in_=tokens_of(grad_out, c))
                 nc.sync.dma_start(out=gates_in[:], in_=tokens_of(gates, c))
-                nc.sync.dma_start(out=hidden_in[:], in_=tokens_of(hidden, c))
                 nc.sync.dma_start(out=hn_in[:], in_=tokens_of(hn, c))
+                nc.sync.dma_start(out=grad_in[:], in_=tokens_of(grad_out, c))
+                nc.sync.dma_start(out=hidden_in[:], in_=tokens_of(hidden, c))
             loaded[c] = {"grad": grad_in, "gates": gates_in, "hidden": hidden_in, "hn": hn_in}
 
-        for c in range(LOADS_AHEAD):
+        for c in range(STREAM_BUFS):
             load_chunk(c)
 
-        nc.vector.tensor_copy(out=w_grouped["n"][:], in_=w_raw["n"][:].rearrange("p t i -> p i t"))
-        nc.vector.tensor_copy(out=w_grouped["r"][:], in_=w_raw["r"][:].rearrange("p t i -> p i t"))
-        half = IN // 2
-        nc.scalar.copy(
-            out=w_grouped["z"][:, :half, :], in_=w_raw["z"][:, :, :half].rearrange("p t i -> p i t")
-        )
-        nc.gpsimd.tensor_scalar(
-            out=w_grouped["z"][:, half:, :],
-            in0=w_raw["z"][:, :, half:].rearrange("p t i -> p i t"),
-            scalar1=1.0,
-            scalar2=0.0,
-            op0=ALU.mult,
-            op1=ALU.add,
-        )
-        for gate in GATES:
-            quantise_weight(gate)
+        def regroup_weight(engine_copy, gate):
+            engine_copy(out=w_grouped[gate][:], in_=w_raw[gate][:].rearrange("p t i -> p i t"))
 
-        made = {}
-        grad_turned = {}
+        regroup_weight(nc.vector.tensor_copy, "n")
+        regroup_weight(nc.vector.tensor_copy, "r")
+        regroup_weight(nc.scalar.copy, "z")
+        quantise_weight("n")
+        idle_codes = const.tile([P, P], U32, align_bytes=64)
+        idle_scales = const.tile([P, P], U8, align_bytes=64)
+        nc.vector.quantize_mx(
+            out=idle_codes[:].bitcast(E5M2X4),
+            scales=idle_scales[:],
+            in_=w_grouped["n"][:].rearrange("p i t -> p (i t)")[:, : P * PACK],
+        )
+        quantise_weight("r")
+        quantise_weight("z")
 
-        def prepare(i):
+        def saved(i, gate):
             c, j = place(i)
-            t = loaded[c]
-            r_in = t["gates"][:, j, 0:H]
-            n_in = t["gates"][:, j, 2 * H : 3 * H]
-            r_sq = natural.tile([P, H], F32)
-            nc.scalar.activation(out=r_sq[:], in_=r_in, func=ACT.Square, bias=-0.5)
-            r_slope = natural.tile([P, H], F32)
+            first = {"r": 0, "z": 1, "n": 2}[gate] * H
+            return loaded[c]["gates"][:, j, first : first + H]
+
+        r_sq = {}
+        n_sq = {}
+        hn_slope = {}
+
+        def square_r(i):
+            r_sq[i] = natural.tile([P, H], F32, name="r_sq")
+            nc.scalar.activation(out=r_sq[i][:], in_=saved(i, "r"), func=ACT.Square, bias=-0.5)
+
+        def square_n(i):
+            n_sq[i] = natural.tile([P, H], F32, name="n_sq")
+            nc.scalar.activation(out=n_sq[i][:], in_=saved(i, "n"), func=ACT.Square)
+
+        def slope(i):
+            c, j = place(i)
+            hn_slope[i] = single.tile([P, H], F32, name="hn_slope")
             nc.gpsimd.tensor_scalar(
-                out=r_slope[:], in0=r_sq[:], scalar1=-1.0, scalar2=0.25, op0=ALU.mult, op1=ALU.add
+                out=hn_slope[i][:], in0=r_sq[i][:], scalar1=-1.0, scalar2=0.25, op0=ALU.mult, op1=ALU.add
             )
-            hn_slope = natural.tile([P, H], F32)
-            nc.gpsimd.tensor_tensor(out=hn_slope[:], in0=t["hn"][:, j, :], in1=r_slope[:], op=ALU.mult)
-            n_sq = natural.tile([P, H], F32)
-            nc.scalar.activation(out=n_sq[:], in_=n_in, func=ACT.Square)
-            made[i] = {"n_sq": n_sq, "hn_slope": hn_slope}
+            nc.gpsimd.tensor_tensor(
+                out=hn_slope[i][:], in0=loaded[c]["hn"][:, j, :], in1=hn_slope[i][:], op=ALU.mult
+            )
+
+        def as_read(bank):
+            return bank[:].rearrange("p t c -> p c t")
+
+        def turn(bank, values):
+            for t in range(PACK):
+                nc.tensor.transpose(bank[:, t, :], values[:, t * P : (t + 1) * P], ident[:])
+
+        z_t = {}
+        n_sq_t = {}
+        slope_t = {}
+        diff_t = {}
+        grad_t = {}
+        grad_banks = []
+
+        def turn_z(i):
+            z_t[i] = psum_z.tile([P, PACK, P], F32, name="z_t")
+            turn(z_t[i], saved(i, "z"))
+
+        def turn_n_sq(i):
+            n_sq_t[i] = psum_one.tile([P, PACK, P], F32, name="n_sq_t")
+            turn(n_sq_t[i], n_sq[i][:])
+
+        def turn_slope(i):
+            slope_t[i] = psum_one.tile([P, PACK, P], F32, name="slope_t")
+            turn(slope_t[i], hn_slope[i][:])
+
+        def turn_n_less_h(i):
+            c, j = place(i)
+            diff_t[i] = psum_one.tile([P, PACK, P], F32, name="diff_t")
+            for t in range(PACK):
+                nc.tensor.matmul(
+                    out=diff_t[i][:, t, :], lhsT=loaded[c]["hidden"][:, j, t * P : (t + 1) * P],
+                    rhs=neg_ident_bf16[:], start=(t == 0), stop=False,
+                )
+            for t in range(PACK):
+                nc.tensor.matmul(
+                    out=diff_t[i][:, t, :], lhsT=saved(i, "n")[:, t * P : (t + 1) * P],
+                    rhs=ident[:], is_transpose=True, start=False, stop=(t == PACK - 1),
+                )
 
         def turn_grad(c):
-            bank = psum_grad.tile([P, CHUNKS[c], PACK, P], BF16)
+            bank = psum_one.tile([P, CHUNKS[c], PACK, P], BF16, name="grad_bank")
             for j in range(CHUNKS[c]):
                 for t in range(PACK):
                     nc.tensor.transpose(
                         bank[:, j, t, :], loaded[c]["grad"][:, j, t * P : (t + 1) * P], ident_bf16[:]
                     )
-            grad_t = turned.tile([P, CHUNKS[c], P, PACK], BF16)
-            nc.scalar.copy(out=grad_t[:], in_=bank[:].rearrange("p j t c -> p j c t"))
-            grad_turned[c] = grad_t
+            grad_banks.append((c, bank))
 
-        def turn(values):
-            bank = psum_turn.tile([P, PACK, P], F32, tag="bank")
-            for t in range(PACK):
-                nc.tensor.transpose(bank[:, t, :], values[:, t * P : (t + 1) * P], ident[:])
-            return bank[:].rearrange("p t c -> p c t")
-
-        def turn_n_less_h(i):
-            c, j = place(i)
-            bank = psum_turn.tile([P, PACK, P], F32, tag="bank")
-            for t in range(PACK):
-                cols = slice(t * P, (t + 1) * P)
-                nc.tensor.matmul(
-                    out=bank[:, t, :], lhsT=loaded[c]["gates"][:, j, 2 * H + t * P : 2 * H + (t + 1) * P],
-                    rhs=ident[:], is_transpose=True, start=True, stop=False,
-                )
-                nc.tensor.matmul(
-                    out=bank[:, t, :], lhsT=loaded[c]["hidden"][:, j, cols], rhs=neg_ident_bf16[:],
-                    start=False, stop=True,
-                )
-            return bank[:].rearrange("p t c -> p c t")
-
-        def z_of(i):
-            c, j = place(i)
-            return loaded[c]["gates"][:, j, H : 2 * H]
+        def copy_grad():
+            for c, bank in grad_banks:
+                grad_t[c] = natural.tile([P, CHUNKS[c], P, PACK], BF16, name="grad_t")
+                nc.scalar.copy(out=grad_t[c][:], in_=bank[:].rearrange("p j t c -> p j c t"))
+            grad_banks.clear()
 
         grouped = {}
         codes = {}
         scales = {}
+        passes = []
+        state = {"run": 0, "written": 0, "quantised": 0}
+        sums = {}
+        finished = []
 
-        def slot(i, gate):
-            g = GROUP_OF[i]
-            return GATES.index(gate) * GROUPS[g] + i - FIRST_OF[g]
+        def unit_of(i, gate):
+            return 3 * i + GATES.index(gate)
 
         def grouped_at(i, gate):
-            s = slot(i, gate)
-            return grouped[GROUP_OF[i]][:, s * H : (s + 1) * H].rearrange("p (c t) -> p c t", t=PACK)
+            u = unit_of(i, gate)
+            b = BLOCK_OF[u]
+            if u == FIRST_UNIT[b]:
+                grouped[b] = packed.tile([P, BLOCKS[b] * H], BF16, name="grouped", align_bytes=64)
+            state["written"] = u + 1
+            s = u - FIRST_UNIT[b]
+            return grouped[b][:, s * H : (s + 1) * H].rearrange("p (c t) -> p c t", t=PACK)
 
-        def quantise(g):
-            n = GROUPS[g]
-            codes[g] = packed.tile([P, 3 * n * P], U32, name="codes", align_bytes=64)
-            scales[g] = packed.tile([P, 3 * n * P], U8, name="scales", align_bytes=64)
-            for a, b in ((0, 2 * n), (2 * n, 3 * n)):
+        def quantise(limit):
+            while state["quantised"] < len(BLOCKS) and FIRST_UNIT[state["quantised"]] + BLOCKS[state["quantised"]] <= limit:
+                b = state["quantised"]
+                codes[b] = packed.tile([P, BLOCKS[b] * P], U32, name="codes", align_bytes=64)
+                scales[b] = packed.tile([P, BLOCKS[b] * P], U8, name="scales", align_bytes=64)
                 nc.vector.quantize_mx(
-                    out=codes[g][:, a * P : b * P].bitcast(E5M2X4),
-                    scales=scales[g][:, a * P : b * P],
-                    in_=grouped[g][:, a * H : b * H],
+                    out=codes[b][:].bitcast(E5M2X4), scales=scales[b][:], in_=grouped[b][:]
+                )
+                passes.extend(range(FIRST_UNIT[b], FIRST_UNIT[b] + BLOCKS[b]))
+                state["quantised"] = b + 1
+
+        def sums_of(m):
+            if m not in sums:
+                if m - 2 in finished:
+                    store_finished()
+                sums[m] = psum_sum.tile([P, IN], F32, name="sums")
+            return sums[m]
+
+        def idle_passes(count):
+            opened = (state["run"] + 2) // 3
+            for k in range(count):
+                nc.tensor.matmul_mx(
+                    out=sums_of(opened)[:],
+                    lhsT=idle_codes[:].bitcast(E5M2X4),
+                    lhsT_scale=idle_scales[:],
+                    rhs=w_codes["n"][:].bitcast(E4M3X4),
+                    rhs_scale=w_scales["n"][:],
+                    start=True,
+                    stop=True,
                 )
 
-        def multiply(i):
-            g = GROUP_OF[i]
-            c, j = place(i)
-            sums = psum_sum.tile([P, IN], F32)
-            for gate in GATES:
-                s = slot(i, gate)
+        def multiply(count, fill=True):
+            ready = passes[state["run"] : state["run"] + count]
+            for u in ready:
+                m, gate = u // 3, GATES[u % 3]
+                b = BLOCK_OF[u]
+                s = u - FIRST_UNIT[b]
                 nc.tensor.matmul_mx(
-                    out=sums[:],
-                    lhsT=codes[g][:, s * P : (s + 1) * P].bitcast(E5M2X4),
-                    lhsT_scale=scales[g][:, s * P : (s + 1) * P],
+                    out=sums_of(m)[:],
+                    lhsT=codes[b][:, s * P : (s + 1) * P].bitcast(E5M2X4),
+                    lhsT_scale=scales[b][:, s * P : (s + 1) * P],
                     rhs=w_codes[gate][:].bitcast(E4M3X4),
                     rhs_scale=w_scales[gate][:],
                     start=(gate == GATES[0]),
                     stop=(gate == GATES[-1]),
                 )
-            result = packed.tile([P, IN], F32, name="result")
-            nc.scalar.copy(out=result[:], in_=sums[:])
-            nc.scalar.dma_start(out=tokens_of(out, c)[:, j, :], in_=result[:])
+                state["run"] = u + 1
+                if gate == GATES[-1]:
+                    finished.append(m)
+            if fill and state["run"] < 3 * TILES:
+                idle_passes(count - len(ready))
 
-        def finish_z(i, bank, neg_az):
-            nc.vector.tensor_tensor(out=grouped_at(i, "z"), in0=bank, in1=neg_az[:], op=ALU.mult)
+        def store_finished():
+            for m in finished:
+                c, j = place(m)
+                result = results.tile([P, IN], F32, name="result")
+                nc.scalar.copy(out=result[:], in_=sums[m][:])
+                nc.scalar.dma_start(out=tokens_of(out, c)[:, j, :], in_=result[:])
+            finished.clear()
 
-        turn_grad(0)
-        prepare(0)
-        banks = {0: {"z": turn(z_of(0))}}
-        banks[0]["n_sq"] = turn(made[0]["n_sq"][:])
-        banks[0]["hn_slope"] = turn(made[0]["hn_slope"][:])
-        banks[0]["n_less_h"] = turn_n_less_h(0)
-        for i in range(1, AHEAD):
-            prepare(i)
-
-        multiplied = 0
-        quantised = 0
-        waiting = {}
-        for i in range(TILES):
-            c, j = place(i)
-            g = GROUP_OF[i]
-            more = i + 1 < TILES
-            if j == 0 and c + LOADS_AHEAD < len(CHUNKS):
-                load_chunk(c + LOADS_AHEAD)
-            if more and place(i + 1)[1] == 0:
-                turn_grad(c + 1)
-            if i + AHEAD < TILES:
-                prepare(i + AHEAD)
-            if i == FIRST_OF[g]:
-                grouped[g] = packed.tile([P, 3 * GROUPS[g] * H], BF16, name="grouped", align_bytes=64)
-            here = banks[i]
-
-            neg_a = turned.tile([P, P, PACK], F32)
-            nc.vector.scalar_tensor_tensor(
-                out=neg_a[:], in0=here["z"], scalar=1.0, in1=grad_turned[c][:, j, :, :],
-                op0=ALU.subtract, op1=ALU.mult,
-            )
-            if i > 0:
-                finish_z(i - 1, banks[i - 1]["n_less_h"], waiting[i - 1])
-            if more:
-                banks[i + 1] = {"z": turn(z_of(i + 1))}
-            dn = turned.tile([P, P, PACK], F32)
-            nc.vector.scalar_tensor_tensor(
-                out=dn[:], in0=here["n_sq"], scalar=1.0, in1=neg_a[:], op0=ALU.subtract, op1=ALU.mult
-            )
-            nc.scalar.copy(out=grouped_at(i, "n"), in_=dn[:])
-            if more:
-                banks[i + 1]["n_sq"] = turn(made[i + 1]["n_sq"][:])
-            if i == FIRST_OF[g] and g > 0:
-                quantise(g - 1)
-                quantised = i
-            for m in range(multiplied, quantised if not more else min(quantised, multiplied + 1)):
-                multiply(m)
-                multiplied = m + 1
-            neg_az = turned.tile([P, P, PACK], F32)
-            nc.vector.tensor_tensor(out=neg_az[:], in0=here["z"], in1=neg_a[:], op=ALU.mult)
-            waiting[i] = neg_az
-            if more:
-                banks[i + 1]["hn_slope"] = turn(made[i + 1]["hn_slope"][:])
-            nc.vector.tensor_tensor(out=grouped_at(i, "r"), in0=here["hn_slope"], in1=dn[:], op=ALU.mult)
-            if more:
-                banks[i + 1]["n_less_h"] = turn_n_less_h(i + 1)
-        finish_z(TILES - 1, banks[TILES - 1]["n_less_h"], waiting[TILES - 1])
-        quantise(len(GROUPS) - 1)
-        for m in range(multiplied, TILES):
-            multiply(m)
+        neg_a = {}
+        neg_az = {}
+        dn = {}
+        ALL = 3 * TILES
+        for i in range(-2, TILES + 1):
+            here = 0 <= i < TILES
+            last_rounds = i >= TILES - 1
+            if here and place(i)[1] == 0 and 1 <= place(i)[0] and place(i)[0] + STREAM_BUFS - 1 < len(CHUNKS):
+                load_chunk(place(i)[0] + STREAM_BUFS - 1)
+            if last_rounds:
+                multiply(ALL, fill=False)
+            elif i >= -1:
+                multiply(1)
+            if here:
+                c, j = place(i)
+                neg_a[i] = turned.tile([P, P, PACK], F32, name="neg_a")
+                nc.vector.scalar_tensor_tensor(
+                    out=neg_a[i][:], in0=as_read(z_t[i]), scalar=1.0, in1=grad_t[c][:, j, :, :],
+                    op0=ALU.subtract, op1=ALU.mult,
+                )
+            if 0 <= i - 1:
+                nc.vector.tensor_tensor(
+                    out=grouped_at(i - 1, "z"), in0=as_read(diff_t[i - 1]), in1=neg_az[i - 1][:], op=ALU.mult
+                )
+            if here:
+                turn_n_less_h(i)
+                dn[i] = turned.tile([P, P, PACK], F32, name="dn")
+                nc.vector.scalar_tensor_tensor(
+                    out=dn[i][:], in0=as_read(n_sq_t[i]), scalar=1.0, in1=neg_a[i][:],
+                    op0=ALU.subtract, op1=ALU.mult,
+                )
+                nc.scalar.copy(out=grouped_at(i, "n"), in_=dn[i][:])
+                copy_grad()
+            if 0 <= i + 1 < TILES:
+                turn_n_sq(i + 1)
+            if here:
+                neg_az[i] = turned.tile([P, P, PACK], F32, name="neg_az")
+                nc.vector.tensor_tensor(out=neg_az[i][:], in0=as_read(z_t[i]), in1=neg_a[i][:], op=ALU.mult)
+            if last_rounds:
+                quantise(state["written"])
+                multiply(ALL, fill=False)
+            elif i >= -1:
+                multiply(2)
+            if here:
+                nc.vector.tensor_tensor(
+                    out=grouped_at(i, "r"), in0=as_read(slope_t[i]), in1=dn[i][:], op=ALU.mult
+                )
+            if 0 <= i + 1 < TILES:
+                turn_slope(i + 1)
+            if 0 <= i + 2 < TILES:
+                if i < 0:
+                    turn_grad(place(i + 2)[0])
+                    copy_grad()
+                square_r(i + 2)
+                store_finished()
+                square_n(i + 2)
+                turn_z(i + 2)
+                if i >= 0 and place(i + 2)[1] == 0:
+                    turn_grad(place(i + 2)[0])
+                slope(i + 2)
+            store_finished()
+            if here and not last_rounds:
+                quantise(state["written"])
+        multiply(ALL, fill=False)
+        store_finished()

@@ -19,8 +19,11 @@ TILES = B // P
 GATES = ("n", "r", "z")
 
 CHUNKS = [1, 1, 1, 1] + [2] * 6
-BLOCKS = [2, 2] + [4] * 10 + [2, 1, 1]
+BLOCKS = [4] * 11 + [2, 1, 1]
 STREAM_BUFS = 5
+FILL = False
+TOP, MID = 3, 0
+GP_TILES = ()
 
 FIRST_TILE = [sum(CHUNKS[:c]) for c in range(len(CHUNKS))]
 CHUNK_OF = [c for c in range(len(CHUNKS)) for j in range(CHUNKS[c])]
@@ -137,17 +140,8 @@ def tile_gru_t_v_kernel(
 
         regroup_weight(nc.vector.tensor_copy, "n")
         regroup_weight(nc.vector.tensor_copy, "r")
-        regroup_weight(nc.scalar.copy, "z")
         quantise_weight("n")
-        idle_codes = const.tile([P, P], U32, align_bytes=64)
-        idle_scales = const.tile([P, P], U8, align_bytes=64)
-        nc.vector.quantize_mx(
-            out=idle_codes[:].bitcast(E5M2X4),
-            scales=idle_scales[:],
-            in_=w_grouped["n"][:].rearrange("p i t -> p (i t)")[:, : P * PACK],
-        )
         quantise_weight("r")
-        quantise_weight("z")
 
         def saved(i, gate):
             c, j = place(i)
@@ -269,19 +263,6 @@ def tile_gru_t_v_kernel(
                 sums[m] = psum_sum.tile([P, IN], F32, name="sums")
             return sums[m]
 
-        def idle_passes(count):
-            opened = (state["run"] + 2) // 3
-            for k in range(count):
-                nc.tensor.matmul_mx(
-                    out=sums_of(opened)[:],
-                    lhsT=idle_codes[:].bitcast(E5M2X4),
-                    lhsT_scale=idle_scales[:],
-                    rhs=w_codes["n"][:].bitcast(E4M3X4),
-                    rhs_scale=w_scales["n"][:],
-                    start=True,
-                    stop=True,
-                )
-
         def multiply(count, fill=True):
             ready = passes[state["run"] : state["run"] + count]
             for u in ready:
@@ -300,8 +281,6 @@ def tile_gru_t_v_kernel(
                 state["run"] = u + 1
                 if gate == GATES[-1]:
                     finished.append(m)
-            if fill and state["run"] < 3 * TILES:
-                idle_passes(count - len(ready))
 
         def store_finished():
             for m in finished:
@@ -311,19 +290,37 @@ def tile_gru_t_v_kernel(
                 nc.scalar.dma_start(out=tokens_of(out, c)[:, j, :], in_=result[:])
             finished.clear()
 
+        slope_s = {}
         neg_a = {}
         neg_az = {}
         dn = {}
         ALL = 3 * TILES
-        for i in range(-2, TILES + 1):
+        square_r(0)
+        turn_grad(0)
+        copy_grad()
+        square_n(0)
+        turn_z(0)
+        slope(0)
+        regroup_weight(nc.scalar.copy, "z")
+        turn_n_sq(0)
+        turn_slope(0)
+        turn_grad(1)
+        copy_grad()
+        square_r(1)
+        square_n(1)
+        turn_z(1)
+        slope(1)
+        for i in range(0, TILES + 1):
             here = 0 <= i < TILES
             last_rounds = i >= TILES - 1
             if here and place(i)[1] == 0 and 1 <= place(i)[0] and place(i)[0] + STREAM_BUFS - 1 < len(CHUNKS):
                 load_chunk(place(i)[0] + STREAM_BUFS - 1)
             if last_rounds:
                 multiply(ALL, fill=False)
-            elif i >= -1:
-                multiply(1)
+            else:
+                multiply(TOP, fill=FILL)
+            if grad_banks and CHUNKS[grad_banks[0][0]] > 1:
+                copy_grad()
             if here:
                 c, j = place(i)
                 neg_a[i] = turned.tile([P, P, PACK], F32, name="neg_a")
@@ -352,26 +349,30 @@ def tile_gru_t_v_kernel(
             if last_rounds:
                 quantise(state["written"])
                 multiply(ALL, fill=False)
-            elif i >= -1:
-                multiply(2)
-            if here:
+            else:
+                multiply(MID, fill=FILL)
+            if here and i in GP_TILES:
+                nc.gpsimd.tensor_tensor(out=grouped_at(i, "r"), in0=slope_s[i][:], in1=dn[i][:], op=ALU.mult)
+            elif here:
                 nc.vector.tensor_tensor(
                     out=grouped_at(i, "r"), in0=as_read(slope_t[i]), in1=dn[i][:], op=ALU.mult
                 )
             if 0 <= i + 1 < TILES:
                 turn_slope(i + 1)
             if 0 <= i + 2 < TILES:
-                if i < 0:
-                    turn_grad(place(i + 2)[0])
-                    copy_grad()
                 square_r(i + 2)
                 store_finished()
                 square_n(i + 2)
+                if i + 1 in GP_TILES:
+                    slope_s[i + 1] = turned.tile([P, P, PACK], F32, name="slope_s")
+                    nc.scalar.copy(out=slope_s[i + 1][:], in_=as_read(slope_t[i + 1]))
                 turn_z(i + 2)
-                if i >= 0 and place(i + 2)[1] == 0:
+                if place(i + 2)[1] == 0:
                     turn_grad(place(i + 2)[0])
                 slope(i + 2)
             store_finished()
+            if i == 0:
+                quantise_weight("z")
             if here and not last_rounds:
                 quantise(state["written"])
         multiply(ALL, fill=False)

@@ -24,6 +24,11 @@ STREAM_BUFS = 5
 FILL = False
 TOP, MID = 3, 0
 GP_TILES = ()
+WEIGHT_BEFORE_CHUNK = {0: "n", 1: "r", 2: "z"}
+
+
+def LAG_LIMIT(i):
+    return 3 * i
 
 FIRST_TILE = [sum(CHUNKS[:c]) for c in range(len(CHUNKS))]
 CHUNK_OF = [c for c in range(len(CHUNKS)) for j in range(CHUNKS[c])]
@@ -93,7 +98,7 @@ def tile_gru_t_v_kernel(
         w_grouped = {}
         w_codes = {}
         w_scales = {}
-        for gate in GATES:
+        def load_weight(gate):
             w_raw[gate] = const.tile([P, PACK, IN], BF16, name="w_raw_%s" % gate)
             nc.sync.dma_start(
                 out=w_raw[gate][:], in_=weight_of[gate].rearrange("(t p) i -> p t i", t=PACK)
@@ -121,27 +126,41 @@ def tile_gru_t_v_kernel(
             hn_in = stream.tile([P, size, H], F32)
             if c == 0:
                 nc.sync.dma_start(out=gates_in[:, :, 0:H], in_=tokens_of(gates, c)[:, :, 0:H])
-                nc.sync.dma_start(out=hn_in[:], in_=tokens_of(hn, c))
                 nc.sync.dma_start(out=grad_in[:], in_=tokens_of(grad_out, c))
                 nc.sync.dma_start(out=gates_in[:, :, H : 3 * H], in_=tokens_of(gates, c)[:, :, H : 3 * H])
+                nc.sync.dma_start(out=hn_in[:], in_=tokens_of(hn, c))
                 nc.sync.dma_start(out=hidden_in[:], in_=tokens_of(hidden, c))
             else:
+                nc.sync.dma_start(out=grad_in[:], in_=tokens_of(grad_out, c))
                 nc.sync.dma_start(out=gates_in[:], in_=tokens_of(gates, c))
                 nc.sync.dma_start(out=hn_in[:], in_=tokens_of(hn, c))
-                nc.sync.dma_start(out=grad_in[:], in_=tokens_of(grad_out, c))
                 nc.sync.dma_start(out=hidden_in[:], in_=tokens_of(hidden, c))
             loaded[c] = {"grad": grad_in, "gates": gates_in, "hidden": hidden_in, "hn": hn_in}
 
         for c in range(STREAM_BUFS):
+            if c in WEIGHT_BEFORE_CHUNK:
+                load_weight(WEIGHT_BEFORE_CHUNK[c])
             load_chunk(c)
 
         def regroup_weight(engine_copy, gate):
             engine_copy(out=w_grouped[gate][:], in_=w_raw[gate][:].rearrange("p t i -> p i t"))
 
+        def regroup_weight_in_halves(gate):
+            half = IN // 2
+            nc.scalar.copy(
+                out=w_grouped[gate][:, :half, :], in_=w_raw[gate][:, :, :half].rearrange("p t i -> p i t")
+            )
+            nc.gpsimd.tensor_scalar(
+                out=w_grouped[gate][:, half:, :],
+                in0=w_raw[gate][:, :, half:].rearrange("p t i -> p i t"),
+                scalar1=1.0,
+                scalar2=0.0,
+                op0=ALU.mult,
+                op1=ALU.add,
+            )
+
         regroup_weight(nc.vector.tensor_copy, "n")
-        regroup_weight(nc.vector.tensor_copy, "r")
         quantise_weight("n")
-        quantise_weight("r")
 
         def saved(i, gate):
             c, j = place(i)
@@ -301,7 +320,7 @@ def tile_gru_t_v_kernel(
         square_n(0)
         turn_z(0)
         slope(0)
-        regroup_weight(nc.scalar.copy, "z")
+        regroup_weight_in_halves("r")
         turn_n_sq(0)
         turn_slope(0)
         turn_grad(1)
@@ -310,6 +329,7 @@ def tile_gru_t_v_kernel(
         square_n(1)
         turn_z(1)
         slope(1)
+        regroup_weight_in_halves("z")
         for i in range(0, TILES + 1):
             here = 0 <= i < TILES
             last_rounds = i >= TILES - 1
@@ -372,8 +392,10 @@ def tile_gru_t_v_kernel(
                 slope(i + 2)
             store_finished()
             if i == 0:
+                quantise_weight("r")
+            if i == 1:
                 quantise_weight("z")
             if here and not last_rounds:
-                quantise(state["written"])
+                quantise(LAG_LIMIT(i))
         multiply(ALL, fill=False)
         store_finished()

@@ -77,7 +77,7 @@ def tile_gru_t_v_kernel(
         const = ctx.enter_context(tc.tile_pool(name="const", bufs=1))
         stream = ctx.enter_context(tc.tile_pool(name="stream", bufs=STREAM_BUFS))
         natural = ctx.enter_context(tc.tile_pool(name="natural", bufs=2))
-        single = ctx.enter_context(tc.tile_pool(name="single", bufs=1))
+        single = ctx.enter_context(tc.tile_pool(name="single", bufs=2))
         turned = ctx.enter_context(tc.tile_pool(name="turned", bufs=3))
         packed = ctx.enter_context(tc.tile_pool(name="packed", bufs=3))
         results = ctx.enter_context(tc.tile_pool(name="results", bufs=4))

from contextlib import ExitStack

import concourse.mybir as mybir
from concourse.masks import make_identity

F32 = mybir.dt.float32
BF16 = mybir.dt.bfloat16
U32 = mybir.dt.uint32
U8 = mybir.dt.uint8
E4M3X4 = mybir.dt.float8_e4m3fn_x4
E5M2X4 = mybir.dt.float8_e5m2_x4
ALU = mybir.AluOpType
ACT = mybir.ActivationFunctionType

P = 128
PACK = 4
B, H, IN = 2048, 512, 512
TILES = B // P
GATES = ("n", "r", "z")

CHUNKS = [1, 1, 1, 1] + [2] * 6
BLOCKS = [4] * 11 + [2, 1, 1]
STREAM_BUFS = 5
FILL = False
TOP, MID = 3, 0
GP_TILES = ()
WEIGHT_BEFORE_CHUNK = {0: "n", 1: "r", 2: "z"}


def LAG_LIMIT(i):
    return 3 * i

FIRST_TILE = [sum(CHUNKS[:c]) for c in range(len(CHUNKS))]
CHUNK_OF = [c for c in range(len(CHUNKS)) for j in range(CHUNKS[c])]
FIRST_UNIT = [sum(BLOCKS[:b]) for b in range(len(BLOCKS))]
BLOCK_OF = [b for b in range(len(BLOCKS)) for u in range(BLOCKS[b])]

FLOPS = 2 * B * 3 * H * IN
BYTES = 2 * (2 * B * H) + 3 * (2 * H * IN) + 4 * (3 * B * H) + 4 * (B * H) + 4 * (B * IN)


def tokens_of(tensor, c):
    rows = tensor[FIRST_TILE[c] * P : (FIRST_TILE[c] + CHUNKS[c]) * P, :]
    return rows.rearrange("(p j) f -> p j f", j=CHUNKS[c])


def place(i):
    return CHUNK_OF[i], i - FIRST_TILE[CHUNK_OF[i]]


def tile_gru_t_v_kernel(
    tc,
    x,
    hidden,
    Wir_w,
    Wir_b,
    Whr_w,
    Whr_b,
    Wiz_w,
    Wiz_b,
    Whz_w,
    Whz_b,
    Win_w,
    Win_b,
    Whn_w,
    Whn_b,
    gates,
    hn,
    grad_out,
    out,
):
    nc = tc.nc
    weight_of = {"r": Wir_w, "z": Wiz_w, "n": Win_w}

    with ExitStack() as ctx:
        ctx.enter_context(tc.manual_schedule())
        const = ctx.enter_context(tc.tile_pool(name="const", bufs=1))
        stream = ctx.enter_context(tc.tile_pool(name="stream", bufs=STREAM_BUFS))
        natural = ctx.enter_context(tc.tile_pool(name="natural", bufs=2))
        single = ctx.enter_context(tc.tile_pool(name="single", bufs=2))
        turned = ctx.enter_context(tc.tile_pool(name="turned", bufs=3))
        packed = ctx.enter_context(tc.tile_pool(name="packed", bufs=3))
        results = ctx.enter_context(tc.tile_pool(name="results", bufs=4))
        psum_z = ctx.enter_context(tc.psum_pool(name="psum_z", bufs=2))
        psum_one = ctx.enter_context(tc.psum_pool(name="psum_one", bufs=1))
        psum_sum = ctx.enter_context(tc.psum_pool(name="psum_sum", bufs=2))

        ident = const.tile([P, P], F32)
        make_identity(nc, ident[:])
        ident_bf16 = const.tile([P, P], BF16)
        make_identity(nc, ident_bf16[:])
        neg_ident_bf16 = const.tile([P, P], BF16)
        nc.vector.tensor_scalar(
            out=neg_ident_bf16[:], in0=ident_bf16[:], scalar1=-1.0, scalar2=0.0, op0=ALU.mult, op1=ALU.add
        )

        w_raw = {}
        w_grouped = {}
        w_codes = {}
        w_scales = {}
        def load_weight(gate):
            w_raw[gate] = const.tile([P, PACK, IN], BF16, name="w_raw_%s" % gate)
            nc.sync.dma_start(
                out=w_raw[gate][:], in_=weight_of[gate].rearrange("(t p) i -> p t i", t=PACK)
            )
            w_grouped[gate] = const.tile(
                [P, IN, PACK], BF16, name="w_grouped_%s" % gate, align_bytes=64
            )

        def quantise_weight(gate):
            w_codes[gate] = const.tile([P, IN], U32, name="w_codes_%s" % gate, align_bytes=64)
            w_scales[gate] = const.tile([P, IN], U8, name="w_scales_%s" % gate, align_bytes=64)
            nc.vector.quantize_mx(
                out=w_codes[gate][:].bitcast(E4M3X4),
                scales=w_scales[gate][:],
                in_=w_grouped[gate][:].rearrange("p i t -> p (i t)"),
            )

        loaded = {}

        def load_chunk(c):
            size = CHUNKS[c]
            grad_in = stream.tile([P, size, H], BF16)
            gates_in = stream.tile([P, size, 3 * H], F32)
            hidden_in = stream.tile([P, size, H], BF16)
            hn_in = stream.tile([P, size, H], F32)
            if c == 0:
                nc.sync.dma_start(out=gates_in[:, :, 0:H], in_=tokens_of(gates, c)[:, :, 0:H])
                nc.sync.dma_start(out=grad_in[:], in_=tokens_of(grad_out, c))
                nc.sync.dma_start(out=gates_in[:, :, H : 3 * H], in_=tokens_of(gates, c)[:, :, H : 3 * H])
                nc.sync.dma_start(out=hn_in[:], in_=tokens_of(hn, c))
                nc.sync.dma_start(out=hidden_in[:], in_=tokens_of(hidden, c))
            else:
                nc.sync.dma_start(out=grad_in[:], in_=tokens_of(grad_out, c))
                nc.sync.dma_start(out=gates_in[:], in_=tokens_of(gates, c))
                nc.sync.dma_start(out=hn_in[:], in_=tokens_of(hn, c))
                nc.sync.dma_start(out=hidden_in[:], in_=tokens_of(hidden, c))
            loaded[c] = {"grad": grad_in, "gates": gates_in, "hidden": hidden_in, "hn": hn_in}

        for c in range(STREAM_BUFS):
            if c in WEIGHT_BEFORE_CHUNK:
                load_weight(WEIGHT_BEFORE_CHUNK[c])
            load_chunk(c)

        def regroup_weight(engine_copy, gate):
            engine_copy(out=w_grouped[gate][:], in_=w_raw[gate][:].rearrange("p t i -> p i t"))

        def regroup_weight_in_halves(gate):
            half = IN // 2
            nc.scalar.copy(
                out=w_grouped[gate][:, :half, :], in_=w_raw[gate][:, :, :half].rearrange("p t i -> p i t")
            )
            nc.gpsimd.tensor_scalar(
                out=w_grouped[gate][:, half:, :],
                in0=w_raw[gate][:, :, half:].rearrange("p t i -> p i t"),
                scalar1=1.0,
                scalar2=0.0,
                op0=ALU.mult,
                op1=ALU.add,
            )

        regroup_weight(nc.vector.tensor_copy, "n")
        quantise_weight("n")

        def saved(i, gate):
            c, j = place(i)
            first = {"r": 0, "z": 1, "n": 2}[gate] * H
            return loaded[c]["gates"][:, j, first : first + H]

        r_sq = {}
        n_sq = {}
        hn_slope = {}

        def square_r(i):
            r_sq[i] = natural.tile([P, H], F32, name="r_sq")
            nc.scalar.activation(out=r_sq[i][:], in_=saved(i, "r"), func=ACT.Square, bias=-0.5)

        def square_n(i):
            n_sq[i] = natural.tile([P, H], F32, name="n_sq")
            nc.scalar.activation(out=n_sq[i][:], in_=saved(i, "n"), func=ACT.Square)

        def slope(i):
            c, j = place(i)
            hn_slope[i] = single.tile([P, H], F32, name="hn_slope")
            nc.gpsimd.tensor_scalar(
                out=hn_slope[i][:], in0=r_sq[i][:], scalar1=-1.0, scalar2=0.25, op0=ALU.mult, op1=ALU.add
            )
            nc.gpsimd.tensor_tensor(
                out=hn_slope[i][:], in0=loaded[c]["hn"][:, j, :], in1=hn_slope[i][:], op=ALU.mult
            )

        def as_read(bank):
            return bank[:].rearrange("p t c -> p c t")

        def turn(bank, values):
            for t in range(PACK):
                nc.tensor.transpose(bank[:, t, :], values[:, t * P : (t + 1) * P], ident[:])

        z_t = {}
        n_sq_t = {}
        slope_t = {}
        diff_t = {}
        grad_t = {}
        grad_banks = []

        def turn_z(i):
            z_t[i] = psum_z.tile([P, PACK, P], F32, name="z_t")
            turn(z_t[i], saved(i, "z"))

        def turn_n_sq(i):
            n_sq_t[i] = psum_one.tile([P, PACK, P], F32, name="n_sq_t")
            turn(n_sq_t[i], n_sq[i][:])

        def turn_slope(i):
            slope_t[i] = psum_one.tile([P, PACK, P], F32, name="slope_t")
            turn(slope_t[i], hn_slope[i][:])

        def turn_n_less_h(i):
            c, j = place(i)
            diff_t[i] = psum_one.tile([P, PACK, P], F32, name="diff_t")
            for t in range(PACK):
                nc.tensor.matmul(
                    out=diff_t[i][:, t, :], lhsT=loaded[c]["hidden"][:, j, t * P : (t + 1) * P],
                    rhs=neg_ident_bf16[:], start=(t == 0), stop=False,
                )
            for t in range(PACK):
                nc.tensor.matmul(
                    out=diff_t[i][:, t, :], lhsT=saved(i, "n")[:, t * P : (t + 1) * P],
                    rhs=ident[:], is_transpose=True, start=False, stop=(t == PACK - 1),
                )

        def turn_grad(c):
            bank = psum_one.tile([P, CHUNKS[c], PACK, P], BF16, name="grad_bank")
            for j in range(CHUNKS[c]):
                for t in range(PACK):
                    nc.tensor.transpose(
                        bank[:, j, t, :], loaded[c]["grad"][:, j, t * P : (t + 1) * P], ident_bf16[:]
                    )
            grad_banks.append((c, bank))

        def copy_grad():
            for c, bank in grad_banks:
                grad_t[c] = natural.tile([P, CHUNKS[c], P, PACK], BF16, name="grad_t")
                nc.scalar.copy(out=grad_t[c][:], in_=bank[:].rearrange("p j t c -> p j c t"))
            grad_banks.clear()

        grouped = {}
        codes = {}
        scales = {}
        passes = []
        state = {"run": 0, "written": 0, "quantised": 0}
        sums = {}
        finished = []

        def unit_of(i, gate):
            return 3 * i + GATES.index(gate)

        def grouped_at(i, gate):
            u = unit_of(i, gate)
            b = BLOCK_OF[u]
            if u == FIRST_UNIT[b]:
                grouped[b] = packed.tile([P, BLOCKS[b] * H], BF16, name="grouped", align_bytes=64)
            state["written"] = u + 1
            s = u - FIRST_UNIT[b]
            return grouped[b][:, s * H : (s + 1) * H].rearrange("p (c t) -> p c t", t=PACK)

        def quantise(limit):
            while state["quantised"] < len(BLOCKS) and FIRST_UNIT[state["quantised"]] + BLOCKS[state["quantised"]] <= limit:
                b = state["quantised"]
                codes[b] = packed.tile([P, BLOCKS[b] * P], U32, name="codes", align_bytes=64)
                scales[b] = packed.tile([P, BLOCKS[b] * P], U8, name="scales", align_bytes=64)
                nc.vector.quantize_mx(
                    out=codes[b][:].bitcast(E5M2X4), scales=scales[b][:], in_=grouped[b][:]
                )
                passes.extend(range(FIRST_UNIT[b], FIRST_UNIT[b] + BLOCKS[b]))
                state["quantised"] = b + 1

        def sums_of(m):
            if m not in sums:
                if m - 2 in finished:
                    store_finished()
                sums[m] = psum_sum.tile([P, IN], F32, name="sums")
            return sums[m]

        def multiply(count, fill=True):
            ready = passes[state["run"] : state["run"] + count]
            for u in ready:
                m, gate = u // 3, GATES[u % 3]
                b = BLOCK_OF[u]
                s = u - FIRST_UNIT[b]
                nc.tensor.matmul_mx(
                    out=sums_of(m)[:],
                    lhsT=codes[b][:, s * P : (s + 1) * P].bitcast(E5M2X4),
                    lhsT_scale=scales[b][:, s * P : (s + 1) * P],
                    rhs=w_codes[gate][:].bitcast(E4M3X4),
                    rhs_scale=w_scales[gate][:],
                    start=(gate == GATES[0]),
                    stop=(gate == GATES[-1]),
                )
                state["run"] = u + 1
                if gate == GATES[-1]:
                    finished.append(m)

        def store_finished():
            for m in finished:
                c, j = place(m)
                result = results.tile([P, IN], F32, name="result")
                nc.scalar.copy(out=result[:], in_=sums[m][:])
                nc.scalar.dma_start(out=tokens_of(out, c)[:, j, :], in_=result[:])
            finished.clear()

        slope_s = {}
        neg_a = {}
        neg_az = {}
        dn = {}
        ALL = 3 * TILES
        square_r(0)
        turn_grad(0)
        copy_grad()
        square_n(0)
        turn_z(0)
        slope(0)
        regroup_weight_in_halves("r")
        turn_n_sq(0)
        turn_slope(0)
        turn_grad(1)
        copy_grad()
        square_r(1)
        square_n(1)
        turn_z(1)
        slope(1)
        regroup_weight_in_halves("z")
        for i in range(0, TILES + 1):
            here = 0 <= i < TILES
            last_rounds = i >= TILES - 1
            if here and place(i)[1] == 0 and 1 <= place(i)[0] and place(i)[0] + STREAM_BUFS - 1 < len(CHUNKS):
                load_chunk(place(i)[0] + STREAM_BUFS - 1)
            if last_rounds:
                multiply(ALL, fill=False)
            else:
                multiply(TOP, fill=FILL)
            if grad_banks and CHUNKS[grad_banks[0][0]] > 1:
                copy_grad()
            if here:
                c, j = place(i)
                neg_a[i] = turned.tile([P, P, PACK], F32, name="neg_a")
                nc.vector.scalar_tensor_tensor(
                    out=neg_a[i][:], in0=as_read(z_t[i]), scalar=1.0, in1=grad_t[c][:, j, :, :],
                    op0=ALU.subtract, op1=ALU.mult,
                )
            if 0 <= i - 1:
                nc.vector.tensor_tensor(
                    out=grouped_at(i - 1, "z"), in0=as_read(diff_t[i - 1]), in1=neg_az[i - 1][:], op=ALU.mult
                )
            if here:
                turn_n_less_h(i)
                dn[i] = turned.tile([P, P, PACK], F32, name="dn")
                nc.vector.scalar_tensor_tensor(
                    out=dn[i][:], in0=as_read(n_sq_t[i]), scalar=1.0, in1=neg_a[i][:],
                    op0=ALU.subtract, op1=ALU.mult,
                )
                nc.scalar.copy(out=grouped_at(i, "n"), in_=dn[i][:])
                copy_grad()
            if 0 <= i + 1 < TILES:
                turn_n_sq(i + 1)
            if here:
                neg_az[i] = turned.tile([P, P, PACK], F32, name="neg_az")
                nc.vector.tensor_tensor(out=neg_az[i][:], in0=as_read(z_t[i]), in1=neg_a[i][:], op=ALU.mult)
            if last_rounds:
                quantise(state["written"])
                multiply(ALL, fill=False)
            else:
                multiply(MID, fill=FILL)
            if here and i in GP_TILES:
                nc.gpsimd.tensor_tensor(out=grouped_at(i, "r"), in0=slope_s[i][:], in1=dn[i][:], op=ALU.mult)
            elif here:
                nc.vector.tensor_tensor(
                    out=grouped_at(i, "r"), in0=as_read(slope_t[i]), in1=dn[i][:], op=ALU.mult
                )
            if 0 <= i + 1 < TILES:
                turn_slope(i + 1)
            if 0 <= i + 2 < TILES:
                square_r(i + 2)
                store_finished()
                square_n(i + 2)
                if i + 1 in GP_TILES:
                    slope_s[i + 1] = turned.tile([P, P, PACK], F32, name="slope_s")
                    nc.scalar.copy(out=slope_s[i + 1][:], in_=as_read(slope_t[i + 1]))
                turn_z(i + 2)
                if place(i + 2)[1] == 0:
                    turn_grad(place(i + 2)[0])
                slope(i + 2)
            store_finished()
            if i == 0:
                quantise_weight("r")
            if i == 1:
                quantise_weight("z")
            if here and not last_rounds:
                quantise(LAG_LIMIT(i))
        multiply(ALL, fill=False)
        store_finished()
